import numpy as np
import ml_dtypes


def mxq(x, axis, fmt="e4m3"):
    dtype, down = {"e4m3": (ml_dtypes.float8_e4m3fn, 7), "e5m2": (ml_dtypes.float8_e5m2, 14)}[fmt]
    v = np.moveaxis(np.asarray(x, np.float32).astype(ml_dtypes.bfloat16).astype(np.float64), axis, -1)
    blocks = v.reshape(v.shape[:-1] + (-1, 32))
    amax = np.abs(blocks).max(-1, keepdims=True)
    byte = np.maximum(np.where(amax > 0, np.frexp(amax)[1] - 1 + 127, 0) - down, 1)
    scale = np.exp2(byte - 127.0)
    codes = (blocks / scale).astype(np.float32).astype(dtype).astype(np.float64)
    return np.moveaxis((codes * scale).reshape(v.shape), -1, axis)


WIDE = False


def mx_kscale(k):
    if not WIDE:
        return np.ones(k)
    levels = np.array([10, -10, 5, -5, 0])
    a = np.random.permutation(np.resize(levels, k // 512 * 4)).reshape(k // 512, 4)
    idx = np.arange(k)
    return np.exp2(a[idx // 512, idx % 128 // 32])


BF16 = ml_dtypes.bfloat16


def bf(x):
    return np.asarray(x, np.float32).astype(BF16)


def f64(x):
    return np.asarray(x).astype(np.float64)


E2M1 = np.array([0.0, 0.5, 1.0, 1.5, 2.0, 3.0, 4.0, 6.0, -0.0, -0.5, -1.0, -1.5, -2.0, -3.0, -4.0, -6.0])


def pack_weight(w, fmt):
    k, n = w.shape
    w = f64(bf(w)).reshape(k // 32, 32, n)
    amax = np.abs(w).max(1)
    if fmt == "e4m3":
        byte = np.frexp(amax)[1] - 1 + 127 - 7
    else:
        mant, ex = np.frexp(amax / 6.0)
        byte = np.where(mant > 0.5, ex, ex - 1) + 127
    byte = np.clip(np.where(amax > 0, byte, 1), 1, 254)
    scaled = (w * np.exp2(127.0 - byte)[:, None, :]).reshape(k, n).astype(np.float32)
    by_word = np.ascontiguousarray(scaled.reshape(k // 512, 128, 4, n).transpose(0, 1, 3, 2))
    if fmt == "e4m3":
        words = by_word.astype(ml_dtypes.float8_e4m3fn).view(np.uint8)
    else:
        c = by_word.astype(ml_dtypes.float4_e2m1fn).view(np.uint8) & 0xF
        words = c[..., 0::2] | (c[..., 1::2] << 4)
    return np.ascontiguousarray(words), np.ascontiguousarray(byte.astype(np.uint8).reshape(k // 512, 16, n))


def unpack_weight(words, scales, fmt):
    g, p, n, _ = words.shape
    if fmt == "e4m3":
        vals = np.ascontiguousarray(words).view(ml_dtypes.float8_e4m3fn).astype(np.float64)
    else:
        nib = np.empty((g, p, n, 4), np.uint8)
        nib[..., 0::2] = words & 0xF
        nib[..., 1::2] = words >> 4
        vals = E2M1[nib]
    vals = vals * np.repeat(np.exp2(scales.astype(np.float64) - 127.0), 8, axis=1)[..., None]
    return vals.transpose(0, 1, 3, 2).reshape(g * 512, n)

def pack4(w):
    words, scales = pack_weight(w, "e2m1")
    return words.reshape(words.shape[0], 128, -1), scales


def unpack4(words, scales):
    return unpack_weight(words.reshape(words.shape[0], 128, -1, 2), scales, "e2m1")


N, DIN, DHID, DOUT, DMLP, NF = 128, 1024, 512, 512, 512, 8
G = 3 * DHID
FS = N // NF
SYNC = 0.15


def sigmoid(v):
    return 1.0 / (1.0 + np.exp(-v))


def setup_inputs():
    s = mx_kscale(DOUT)
    o = np.random.standard_normal((N, DOUT)) * (0.8 + 0.8 * np.random.random((N, 1)))
    rows = np.concatenate([0.55 / np.sqrt(DOUT) / s, np.array([0.3])])
    eng_out = bf(o * s)
    tension = bf((o * o).mean(-1))
    hiddens = bf(np.random.standard_normal((N, DHID)) * (0.5 + np.random.random((N, 1))))
    w_ih = bf(np.random.standard_normal((DOUT + 1, G)) * rows[:, None])
    b_ih = bf(np.random.standard_normal(G) * 0.3)
    w_hh_words, w_hh_scales = pack4(np.random.standard_normal((DHID, G)) * 0.7 / np.sqrt(DHID))
    b_hh = bf(np.random.standard_normal(G) * 0.3)
    return {
        "eng_out": eng_out,
        "tension": tension,
        "hiddens": hiddens,
        "w_ih": w_ih,
        "b_ih": b_ih,
        "w_hh_words": w_hh_words,
        "w_hh_scales": w_hh_scales,
        "b_hh": b_hh,
    }


def reference(eng_out, tension, hiddens, w_ih, b_ih, w_hh_words, w_hh_scales, b_hh):
    h = f64(hiddens)
    wi = f64(w_ih)
    gi = (mxq(f64(eng_out), 1, "e4m3") @ mxq(wi[:DOUT], 0, "e4m3")) + f64(tension)[:, None] * wi[DOUT] + f64(b_ih)
    gh = (mxq(h, 1, "e4m3") @ unpack4(w_hh_words, w_hh_scales)) + f64(b_hh)
    ir, iz, inn = np.split(gi, 3, axis=-1)
    hr, hz, hn = np.split(gh, 3, axis=-1)
    r = sigmoid(ir + hr)
    z = sigmoid(iz + hz)
    ncand = np.tanh(inn + r * hn)
    h_new = (1.0 - z) * ncand + z * h
    hf = h_new.reshape(NF, FS, DHID)
    fmean = hf.mean(axis=1, keepdims=True)
    hf = (1.0 - SYNC) * hf + SYNC * fmean
    return hf.reshape(N, DHID)

@@ -1,0 +1,295 @@
+from contextlib import ExitStack
+
+import concourse.mybir as mybir
+from concourse.masks import make_identity
+
+F32 = mybir.dt.float32
+BF16 = mybir.dt.bfloat16
+I32 = mybir.dt.int32
+U32 = mybir.dt.uint32
+U8 = mybir.dt.uint8
+FP8X4 = mybir.dt.float8_e4m3fn_x4
+FP4X4 = mybir.dt.float4_e2m1fn_x4
+ADD = mybir.AluOpType.add
+MULT = mybir.AluOpType.mult
+ACT = mybir.ActivationFunctionType
+
+P = 128
+PACK = 4
+CELLS = 128
+HID = 512
+GATES = 3
+R, Z, N = 0, 1, 2
+BLOCK = 128
+BLOCKS = HID // BLOCK
+FACTION = 16
+SYNC = 0.15
+ENG, HIDDEN = 0, 1
+HALVES = 2
+HALF = HID // HALVES
+HALF_BLOCKS = HALF // BLOCK
+
+FLOPS = 2 * CELLS * (HID + 1 + HID) * GATES * HID
+
+
+def tile_fractalengine_pb_s_kernel(
+    tc, eng_out, tension, hiddens, w_ih, b_ih, w_hh_words, w_hh_scales, b_hh, out
+):
+    nc = tc.nc
+    with ExitStack() as ctx:
+        keep = ctx.enter_context(tc.tile_pool(name="keep", bufs=1))
+        psum = ctx.enter_context(tc.psum_pool(name="psum", bufs=1))
+        ctx.enter_context(tc.manual_schedule())
+
+        ident_f32 = keep.tile([P, P], F32)
+        make_identity(nc, ident_f32[:])
+        whh_scales = keep.tile([P, GATES * HID], U8, align_bytes=64)
+        nc.vector.memset(whh_scales[:].bitcast(I32), 0)
+        rows = keep.tile([P, P], BF16)
+        nc.vector.memset(rows[:], 0.0)
+        warm = keep.tile([P, 2], F32)
+        nc.vector.memset(warm[:], 0.0)
+        ident_bf16 = keep.tile([P, P], BF16)
+        nc.vector.tensor_copy(out=ident_bf16[:], in_=ident_f32[:])
+
+        x_sb = keep.tile([P, 2, HID], BF16)
+        nc.sync.dma_start(out=x_sb[:, ENG, :], in_=eng_out)
+        nc.sync.dma_start(out=x_sb[:, HIDDEN, :], in_=hiddens)
+
+        n_rows = GATES * BLOCKS
+        tension_bc = keep.tile([P, CELLS], BF16)
+        nc.scalar.dma_start(out=tension_bc[:], in_=tension.partition_broadcast(P))
+        nc.scalar.dma_start(
+            out=rows[2 * n_rows : 3 * n_rows, :],
+            in_=w_ih[HID : HID + 1, :].rearrange("o (q m) -> (o q) m", m=BLOCK),
+        )
+        nc.scalar.dma_start(out=rows[0:n_rows, :], in_=b_ih.rearrange("(q m) -> q m", m=BLOCK))
+        nc.scalar.dma_start(out=rows[n_rows : 2 * n_rows, :], in_=b_hh.rearrange("(q m) -> q m", m=BLOCK))
+
+        raw = {}
+
+        def load_columns(g, halves):
+            width = len(halves) * HALF
+            first = g * HID + halves[0] * HALF
+            loaded = keep.tile([P, PACK, width], BF16, name="raw%d%d" % (g, halves[0]))
+            nc.sync.dma_start(
+                out=loaded[:], in_=w_ih[0:HID, first : first + width].rearrange("(p t) w -> p t w", t=PACK)
+            )
+            for i, half in enumerate(halves):
+                raw[(g, half)] = loaded[:, :, i * HALF : (i + 1) * HALF]
+
+        load_columns(R, (0, 1))
+        whh_words = keep.tile([P, 2 * GATES * HID], U8, align_bytes=64)
+        nc.sync.dma_start(
+            out=whh_words[:].bitcast(I32), in_=w_hh_words.rearrange("g p b -> (g p) b").bitcast(I32)
+        )
+        for quadrant in range(4):
+            nc.sync.dma_start(
+                out=whh_scales[32 * quadrant : 32 * quadrant + 4, :].bitcast(I32),
+                in_=w_hh_scales[0, 4 * quadrant : 4 * quadrant + 4, :].bitcast(I32),
+            )
+        load_columns(Z, (0, 1))
+        load_columns(N, (0,))
+        load_columns(N, (1,))
+        nc.scalar.activation(out=warm[:, 1:2], in_=warm[:, 0:1], func=ACT.Sigmoid)
+
+        xt_ps = psum.tile([P, 2, 2, CELLS], F32)
+        x_words = x_sb[:].bitcast(F32)
+        for a in (ENG, HIDDEN):
+            for u in range(2):
+                nc.tensor.transpose(xt_ps[:, a, u, :], x_words[:, a, u : HID // 2 : 2], ident_f32[:])
+        x_grouped = keep.tile([P, 2, CELLS, PACK], BF16, align_bytes=64)
+        nc.scalar.copy(out=x_grouped[:].bitcast(F32), in_=xt_ps[:].rearrange("p a u c -> p a c u"))
+        x_codes = keep.tile([P, 2 * CELLS], U32, align_bytes=64)
+        x_scales = keep.tile([P, 2 * CELLS], U8, align_bytes=64)
+        nc.vector.quantize_mx(
+            out=x_codes[:].bitcast(FP8X4),
+            scales=x_scales[:],
+            in_=x_grouped[:].rearrange("p a c t -> p (a c t)"),
+        )
+
+        ht_ps = psum.tile([P, BLOCKS, CELLS], BF16)
+        for j in range(BLOCKS):
+            nc.tensor.transpose(ht_ps[:, j, :], x_sb[:, HIDDEN, j * BLOCK : (j + 1) * BLOCK], ident_bf16[:])
+
+        rows_ps = psum.tile([P, P], BF16)
+        nc.tensor.transpose(rows_ps[:], rows[:], ident_bf16[:])
+        cols = keep.tile([P, 3 * n_rows], F32)
+        nc.vector.tensor_copy(out=cols[:], in_=rows_ps[:, 0 : 3 * n_rows])
+        both = 2 * BLOCKS
+        nc.vector.tensor_add(out=cols[:, 0:both], in0=cols[:, 0:both], in1=cols[:, n_rows : n_rows + both])
+        minus_bias_z = keep.tile([P, BLOCKS], F32)
+        nc.vector.tensor_scalar_mul(out=minus_bias_z[:], in0=cols[:, Z * BLOCKS : (Z + 1) * BLOCKS], scalar1=-1.0)
+
+        def bias(g, j):
+            return cols[:, g * BLOCKS + j : g * BLOCKS + j + 1]
+
+        def bias_hn(j):
+            return cols[:, n_rows + N * BLOCKS + j : n_rows + N * BLOCKS + j + 1]
+
+        def last_row(g, j):
+            return cols[:, 2 * n_rows + g * BLOCKS + j : 2 * n_rows + g * BLOCKS + j + 1]
+
+        grouped = keep.tile([P, GATES * HID, PACK], BF16, align_bytes=64)
+        wih_codes = keep.tile([P, GATES * HID], U32, align_bytes=64)
+        wih_scales = keep.tile([P, GATES * HID], U8, align_bytes=64)
+        half_copy = (nc.vector.tensor_copy, nc.scalar.copy)
+
+        def regroup(g, half):
+            piece = slice(g * HID + half * HALF, g * HID + (half + 1) * HALF)
+            half_copy[half](
+                out=grouped[:, piece, :].rearrange("p (c i) t -> p c t i", i=4),
+                in_=raw[(g, half)].rearrange("p t (c i) -> p c t i", i=4),
+            )
+
+        def quantise(g, half):
+            piece = slice(g * HID + half * HALF, g * HID + (half + 1) * HALF)
+            nc.vector.quantize_mx(
+                out=wih_codes[:, piece].bitcast(FP8X4),
+                scales=wih_scales[:, piece],
+                in_=grouped[:, piece, :].rearrange("p w t -> p (w t)"),
+            )
+
+        def pass_hh(acc, g, j, start, stop):
+            col = g * HID + j * BLOCK
+            nc.tensor.matmul_mx(
+                out=acc,
+                lhsT=whh_words[:, 2 * col : 2 * (col + BLOCK)].bitcast(FP4X4),
+                lhsT_scale=whh_scales[:, col : col + BLOCK],
+                rhs=x_codes[:, CELLS : 2 * CELLS].bitcast(FP8X4),
+                rhs_scale=x_scales[:, CELLS : 2 * CELLS],
+                start=start,
+                stop=stop,
+            )
+
+        def pass_ih(acc, g, j, start, stop):
+            col = g * HID + j * BLOCK
+            nc.tensor.matmul_mx(
+                out=acc,
+                lhsT=wih_codes[:, col : col + BLOCK].bitcast(FP8X4),
+                lhsT_scale=wih_scales[:, col : col + BLOCK],
+                rhs=x_codes[:, 0:CELLS].bitcast(FP8X4),
+                rhs_scale=x_scales[:, 0:CELLS],
+                start=start,
+                stop=stop,
+            )
+
+        whole = [P, BLOCKS, CELLS]
+        acc = [psum.tile(whole, F32, name="acc%d" % g) for g in (R, Z)]
+        pre = [keep.tile(whole, F32, name="pre%d" % g) for g in (R, Z)]
+        hn_ps = psum.tile(whole, F32)
+        in_ps = [psum.tile([P, HALF_BLOCKS, CELLS], F32, name="in%d" % half) for half in range(HALVES)]
+        r = keep.tile(whole, F32)
+        rh = keep.tile(whole, F32)
+        rest_n = keep.tile(whole, F32)
+        z = keep.tile(whole, F32)
+        one_minus_z = keep.tile(whole, F32)
+        zh = keep.tile(whole, F32)
+        pre_n = keep.tile(whole, F32)
+        n_cand = keep.tile(whole, F32)
+        fresh = keep.tile(whole, F32)
+        h_new = keep.tile(whole, F32)
+        mixed = keep.tile(whole, F32)
+        fsum = keep.tile([P, BLOCKS * CELLS // FACTION], F32)
+        out_sb = keep.tile([P, HID], F32)
+
+        def blocks_of(half):
+            return range(half * HALF_BLOCKS, (half + 1) * HALF_BLOCKS)
+
+        def passes_hn():
+            for j in range(BLOCKS):
+                pass_hh(hn_ps[:, j, :], N, j, True, True)
+
+        def passes_both(g):
+            for j in range(BLOCKS):
+                pass_hh(acc[g][:, j, :], g, j, True, False)
+                pass_ih(acc[g][:, j, :], g, j, False, True)
+
+        def passes_in(half):
+            for b, j in enumerate(blocks_of(half)):
+                pass_ih(in_ps[half][:, b, :], N, j, True, True)
+
+        def add_tension(g):
+            for j in range(BLOCKS):
+                nc.vector.scalar_tensor_tensor(
+                    out=pre[g][:, j, :], in0=tension_bc[:], scalar=last_row(g, j), in1=acc[g][:, j, :], op0=MULT, op1=ADD
+                )
+
+        def sigmoid(dst, g, sign, biases):
+            for j in range(BLOCKS):
+                nc.scalar.activation(
+                    out=dst[:, j, :], in_=pre[g][:, j, :], func=ACT.Sigmoid, scale=sign, bias=biases[:, j : j + 1]
+                )
+
+        def r_times_hn():
+            for j in range(BLOCKS):
+                nc.vector.scalar_tensor_tensor(
+                    out=rh[:, j, :], in0=hn_ps[:, j, :], scalar=bias_hn(j), in1=r[:, j, :], op0=ADD, op1=MULT
+                )
+
+        def rest_of_n():
+            for j in range(BLOCKS):
+                nc.vector.scalar_tensor_tensor(
+                    out=rest_n[:, j, :], in0=tension_bc[:], scalar=last_row(N, j), in1=rh[:, j, :], op0=MULT, op1=ADD
+                )
+
+        def candidate(half):
+            of_half = slice(half * HALF_BLOCKS, (half + 1) * HALF_BLOCKS)
+            nc.vector.tensor_add(out=pre_n[:, of_half, :], in0=in_ps[half][:], in1=rest_n[:, of_half, :])
+            for j in blocks_of(half):
+                nc.scalar.activation(out=n_cand[:, j, :], in_=pre_n[:, j, :], func=ACT.Tanh, bias=bias(N, j))
+
+        def finish(half):
+            of_half = slice(half * HALF_BLOCKS, (half + 1) * HALF_BLOCKS)
+            by_faction = "p b (f i) -> p (b f) i"
+            factions = HALF_BLOCKS * CELLS // FACTION
+            sums = fsum[:, half * factions : (half + 1) * factions]
+            nc.vector.tensor_mul(out=fresh[:, of_half, :], in0=one_minus_z[:, of_half, :], in1=n_cand[:, of_half, :])
+            nc.vector.tensor_add(out=h_new[:, of_half, :], in0=fresh[:, of_half, :], in1=zh[:, of_half, :])
+            nc.vector.tensor_reduce(
+                out=sums, in_=h_new[:, of_half, :].rearrange(by_faction, i=FACTION), axis=mybir.AxisListType.X, op=ADD
+            )
+            nc.vector.scalar_tensor_tensor(
+                out=mixed[:, of_half, :].rearrange(by_faction, i=FACTION),
+                in0=sums.unsqueeze(2).to_broadcast([P, factions, FACTION]),
+                scalar=SYNC / (1.0 - SYNC) / FACTION,
+                in1=h_new[:, of_half, :].rearrange(by_faction, i=FACTION),
+                op0=MULT,
+                op1=ADD,
+            )
+            back_ps = psum.tile([P, HALF_BLOCKS, BLOCK], F32, tag="acc%d" % half, name="back%d" % half)
+            for b, j in enumerate(blocks_of(half)):
+                nc.tensor.transpose(back_ps[:, b, :], mixed[:, j, :], ident_f32[:])
+            cols_of = slice(half * HALF, (half + 1) * HALF)
+            nc.scalar.mul(out=out_sb[:, cols_of], in_=back_ps[:].rearrange("p b m -> p (b m)"), mul=1.0 - SYNC)
+            nc.sync.dma_start(out=out[:, cols_of], in_=out_sb[:, cols_of])
+
+        regroup(R, 0)
+        regroup(R, 1)
+        quantise(R, 0)
+        quantise(R, 1)
+        passes_hn()
+        passes_both(R)
+        regroup(Z, 0)
+        regroup(Z, 1)
+        add_tension(R)
+        sigmoid(r, R, 1.0, cols[:, R * BLOCKS : (R + 1) * BLOCKS])
+        quantise(Z, 0)
+        quantise(Z, 1)
+        passes_both(Z)
+        regroup(N, 0)
+        regroup(N, 1)
+        r_times_hn()
+        quantise(N, 0)
+        passes_in(0)
+        add_tension(Z)
+        sigmoid(z, Z, 1.0, cols[:, Z * BLOCKS : (Z + 1) * BLOCKS])
+        sigmoid(one_minus_z, Z, -1.0, minus_bias_z)
+        rest_of_n()
+        quantise(N, 1)
+        passes_in(1)
+        candidate(0)
+        nc.vector.tensor_mul(out=zh[:], in0=z[:], in1=ht_ps[:])
+        candidate(1)
+        finish(0)
+        finish(1)

@@ -56,15 +56,11 @@ def tile_fractalengine_pb_s_kernel(
         nc.sync.dma_start(out=x_sb[:, ENG, :], in_=eng_out)
         nc.sync.dma_start(out=x_sb[:, HIDDEN, :], in_=hiddens)
 
-        n_rows = GATES * BLOCKS
-        tension_bc = keep.tile([P, CELLS], BF16)
-        nc.scalar.dma_start(out=tension_bc[:], in_=tension.partition_broadcast(P))
-        nc.scalar.dma_start(
-            out=rows[2 * n_rows : 3 * n_rows, :],
-            in_=w_ih[HID : HID + 1, :].rearrange("o (q m) -> (o q) m", m=BLOCK),
-        )
-        nc.scalar.dma_start(out=rows[0:n_rows, :], in_=b_ih.rearrange("(q m) -> q m", m=BLOCK))
-        nc.scalar.dma_start(out=rows[n_rows : 2 * n_rows, :], in_=b_hh.rearrange("(q m) -> q m", m=BLOCK))
+        for quadrant in range(4):
+            nc.sync.dma_start(
+                out=whh_scales[32 * quadrant : 32 * quadrant + 4, :].bitcast(I32),
+                in_=w_hh_scales[0, 4 * quadrant : 4 * quadrant + 4, :].bitcast(I32),
+            )
 
         raw = {}
 
@@ -83,11 +79,15 @@ def tile_fractalengine_pb_s_kernel(
         nc.sync.dma_start(
             out=whh_words[:].bitcast(I32), in_=w_hh_words.rearrange("g p b -> (g p) b").bitcast(I32)
         )
-        for quadrant in range(4):
-            nc.sync.dma_start(
-                out=whh_scales[32 * quadrant : 32 * quadrant + 4, :].bitcast(I32),
-                in_=w_hh_scales[0, 4 * quadrant : 4 * quadrant + 4, :].bitcast(I32),
-            )
+        n_rows = GATES * BLOCKS
+        tension_bc = keep.tile([P, CELLS], BF16)
+        nc.scalar.dma_start(out=tension_bc[:], in_=tension.partition_broadcast(P))
+        nc.scalar.dma_start(
+            out=rows[2 * n_rows : 3 * n_rows, :],
+            in_=w_ih[HID : HID + 1, :].rearrange("o (q m) -> (o q) m", m=BLOCK),
+        )
+        nc.scalar.dma_start(out=rows[0:n_rows, :], in_=b_ih.rearrange("(q m) -> q m", m=BLOCK))
+        nc.scalar.dma_start(out=rows[n_rows : 2 * n_rows, :], in_=b_hh.rearrange("(q m) -> q m", m=BLOCK))
         load_columns(Z, (0, 1))
         load_columns(N, (0,))
         load_columns(N, (1,))
@@ -111,15 +111,31 @@ def tile_fractalengine_pb_s_kernel(
         ht_ps = psum.tile([P, BLOCKS, CELLS], BF16)
         for j in range(BLOCKS):
             nc.tensor.transpose(ht_ps[:, j, :], x_sb[:, HIDDEN, j * BLOCK : (j + 1) * BLOCK], ident_bf16[:])
+        ht_sb = keep.tile([P, BLOCKS, CELLS], BF16)
+        nc.scalar.copy(out=ht_sb[:], in_=ht_ps[:])
 
         rows_ps = psum.tile([P, P], BF16)
-        nc.tensor.transpose(rows_ps[:], rows[:], ident_bf16[:])
         cols = keep.tile([P, 3 * n_rows], F32)
-        nc.vector.tensor_copy(out=cols[:], in_=rows_ps[:, 0 : 3 * n_rows])
-        both = 2 * BLOCKS
-        nc.vector.tensor_add(out=cols[:, 0:both], in0=cols[:, 0:both], in1=cols[:, n_rows : n_rows + both])
         minus_bias_z = keep.tile([P, BLOCKS], F32)
-        nc.vector.tensor_scalar_mul(out=minus_bias_z[:], in0=cols[:, Z * BLOCKS : (Z + 1) * BLOCKS], scalar1=-1.0)
+        tension_n = keep.tile([P, BLOCKS, CELLS], F32)
+
+        def small_vectors():
+            nc.tensor.transpose(rows_ps[:], rows[:], ident_bf16[:])
+            nc.vector.tensor_copy(out=cols[:], in_=rows_ps[:, 0 : 3 * n_rows])
+            both = 2 * BLOCKS
+            nc.vector.tensor_add(out=cols[:, 0:both], in0=cols[:, 0:both], in1=cols[:, n_rows : n_rows + both])
+            nc.vector.tensor_scalar_mul(
+                out=minus_bias_z[:], in0=cols[:, Z * BLOCKS : (Z + 1) * BLOCKS], scalar1=-1.0
+            )
+            for j in range(BLOCKS):
+                nc.gpsimd.tensor_scalar(
+                    out=tension_n[:, j, :],
+                    in0=tension_bc[:],
+                    scalar1=last_row(N, j),
+                    scalar2=bias(N, j),
+                    op0=MULT,
+                    op1=ADD,
+                )
 
         def bias(g, j):
             return cols[:, g * BLOCKS + j : g * BLOCKS + j + 1]
@@ -227,40 +243,57 @@ def tile_fractalengine_pb_s_kernel(
                     out=rh[:, j, :], in0=hn_ps[:, j, :], scalar=bias_hn(j), in1=r[:, j, :], op0=ADD, op1=MULT
                 )
 
-        def rest_of_n():
-            for j in range(BLOCKS):
-                nc.vector.scalar_tensor_tensor(
-                    out=rest_n[:, j, :], in0=tension_bc[:], scalar=last_row(N, j), in1=rh[:, j, :], op0=MULT, op1=ADD
-                )
+        def half_of(half):
+            return slice(half * HALF_BLOCKS, (half + 1) * HALF_BLOCKS)
+
+        def rest_of_n(half):
+            nc.gpsimd.tensor_add(
+                out=rest_n[:, half_of(half), :], in0=rh[:, half_of(half), :], in1=tension_n[:, half_of(half), :]
+            )
+
+        def z_times_h(half):
+            nc.gpsimd.tensor_mul(out=zh[:, half_of(half), :], in0=z[:, half_of(half), :], in1=ht_sb[:, half_of(half), :])
 
         def candidate(half):
-            of_half = slice(half * HALF_BLOCKS, (half + 1) * HALF_BLOCKS)
-            nc.vector.tensor_add(out=pre_n[:, of_half, :], in0=in_ps[half][:], in1=rest_n[:, of_half, :])
-            for j in blocks_of(half):
-                nc.scalar.activation(out=n_cand[:, j, :], in_=pre_n[:, j, :], func=ACT.Tanh, bias=bias(N, j))
+            nc.vector.tensor_add(out=pre_n[:, half_of(half), :], in0=in_ps[half][:], in1=rest_n[:, half_of(half), :])
+            nc.scalar.activation(out=n_cand[:, half_of(half), :], in_=pre_n[:, half_of(half), :], func=ACT.Tanh)
 
-        def finish(half):
-            of_half = slice(half * HALF_BLOCKS, (half + 1) * HALF_BLOCKS)
-            by_faction = "p b (f i) -> p (b f) i"
-            factions = HALF_BLOCKS * CELLS // FACTION
-            sums = fsum[:, half * factions : (half + 1) * factions]
-            nc.vector.tensor_mul(out=fresh[:, of_half, :], in0=one_minus_z[:, of_half, :], in1=n_cand[:, of_half, :])
-            nc.vector.tensor_add(out=h_new[:, of_half, :], in0=fresh[:, of_half, :], in1=zh[:, of_half, :])
-            nc.vector.tensor_reduce(
-                out=sums, in_=h_new[:, of_half, :].rearrange(by_faction, i=FACTION), axis=mybir.AxisListType.X, op=ADD
+        def keep_fresh(half):
+            nc.vector.tensor_mul(
+                out=fresh[:, half_of(half), :], in0=one_minus_z[:, half_of(half), :], in1=n_cand[:, half_of(half), :]
             )
+
+        def new_state(half):
+            nc.vector.tensor_add(
+                out=h_new[:, half_of(half), :], in0=fresh[:, half_of(half), :], in1=zh[:, half_of(half), :]
+            )
+
+        by_faction = "p b (f i) -> p (b f) i"
+        factions = HALF_BLOCKS * CELLS // FACTION
+
+        def faction_sums(half):
+            nc.vector.tensor_reduce(
+                out=fsum[:, half * factions : (half + 1) * factions],
+                in_=h_new[:, half_of(half), :].rearrange(by_faction, i=FACTION),
+                axis=mybir.AxisListType.X,
+                op=ADD,
+            )
+
+        def pull(half):
             nc.vector.scalar_tensor_tensor(
-                out=mixed[:, of_half, :].rearrange(by_faction, i=FACTION),
-                in0=sums.unsqueeze(2).to_broadcast([P, factions, FACTION]),
+                out=mixed[:, half_of(half), :].rearrange(by_faction, i=FACTION),
+                in0=fsum[:, half * factions : (half + 1) * factions].unsqueeze(2).to_broadcast([P, factions, FACTION]),
                 scalar=SYNC / (1.0 - SYNC) / FACTION,
-                in1=h_new[:, of_half, :].rearrange(by_faction, i=FACTION),
+                in1=h_new[:, half_of(half), :].rearrange(by_faction, i=FACTION),
                 op0=MULT,
                 op1=ADD,
             )
+
+        def store(half):
+            cols_of = slice(half * HALF, (half + 1) * HALF)
             back_ps = psum.tile([P, HALF_BLOCKS, BLOCK], F32, tag="acc%d" % half, name="back%d" % half)
             for b, j in enumerate(blocks_of(half)):
                 nc.tensor.transpose(back_ps[:, b, :], mixed[:, j, :], ident_f32[:])
-            cols_of = slice(half * HALF, (half + 1) * HALF)
             nc.scalar.mul(out=out_sb[:, cols_of], in_=back_ps[:].rearrange("p b m -> p (b m)"), mul=1.0 - SYNC)
             nc.sync.dma_start(out=out[:, cols_of], in_=out_sb[:, cols_of])
 
@@ -268,6 +301,7 @@ def tile_fractalengine_pb_s_kernel(
         regroup(R, 1)
         quantise(R, 0)
         quantise(R, 1)
+        small_vectors()
         passes_hn()
         passes_both(R)
         regroup(Z, 0)
@@ -277,19 +311,27 @@ def tile_fractalengine_pb_s_kernel(
         quantise(Z, 0)
         quantise(Z, 1)
         passes_both(Z)
+        r_times_hn()
+        rest_of_n(0)
+        rest_of_n(1)
         regroup(N, 0)
         regroup(N, 1)
-        r_times_hn()
-        quantise(N, 0)
-        passes_in(0)
         add_tension(Z)
         sigmoid(z, Z, 1.0, cols[:, Z * BLOCKS : (Z + 1) * BLOCKS])
+        z_times_h(0)
+        z_times_h(1)
         sigmoid(one_minus_z, Z, -1.0, minus_bias_z)
-        rest_of_n()
-        quantise(N, 1)
-        passes_in(1)
-        candidate(0)
-        nc.vector.tensor_mul(out=zh[:], in0=z[:], in1=ht_ps[:])
-        candidate(1)
-        finish(0)
-        finish(1)
+        for half in range(HALVES):
+            quantise(N, half)
+            passes_in(half)
+        for half in range(HALVES):
+            candidate(half)
+        for half in range(HALVES):
+            keep_fresh(half)
+        for half in range(HALVES):
+            new_state(half)
+        for half in range(HALVES):
+            faction_sums(half)
+        for half in range(HALVES):
+            pull(half)
+            store(half)

@@ -56,11 +56,14 @@ def tile_fractalengine_pb_s_kernel(
         nc.sync.dma_start(out=x_sb[:, ENG, :], in_=eng_out)
         nc.sync.dma_start(out=x_sb[:, HIDDEN, :], in_=hiddens)
 
-        for quadrant in range(4):
+        def load_scale_rows(quadrant):
             nc.sync.dma_start(
                 out=whh_scales[32 * quadrant : 32 * quadrant + 4, :].bitcast(I32),
                 in_=w_hh_scales[0, 4 * quadrant : 4 * quadrant + 4, :].bitcast(I32),
             )
+
+        for quadrant in range(3):
+            load_scale_rows(quadrant)
 
         raw = {}
 
@@ -79,6 +82,8 @@ def tile_fractalengine_pb_s_kernel(
         nc.sync.dma_start(
             out=whh_words[:].bitcast(I32), in_=w_hh_words.rearrange("g p b -> (g p) b").bitcast(I32)
         )
+        load_columns(Z, (0, 1))
+        load_scale_rows(3)
         n_rows = GATES * BLOCKS
         tension_bc = keep.tile([P, CELLS], BF16)
         nc.scalar.dma_start(out=tension_bc[:], in_=tension.partition_broadcast(P))
@@ -86,11 +91,11 @@ def tile_fractalengine_pb_s_kernel(
             out=rows[2 * n_rows : 3 * n_rows, :],
             in_=w_ih[HID : HID + 1, :].rearrange("o (q m) -> (o q) m", m=BLOCK),
         )
-        nc.scalar.dma_start(out=rows[0:n_rows, :], in_=b_ih.rearrange("(q m) -> q m", m=BLOCK))
-        nc.scalar.dma_start(out=rows[n_rows : 2 * n_rows, :], in_=b_hh.rearrange("(q m) -> q m", m=BLOCK))
-        load_columns(Z, (0, 1))
         load_columns(N, (0,))
         load_columns(N, (1,))
+        nc.gpsimd.dma_start(out=rows[0:n_rows, :], in_=b_ih.rearrange("(q m) -> q m", m=BLOCK))
+        nc.gpsimd.dma_start(out=rows[n_rows : 2 * n_rows, :], in_=b_hh.rearrange("(q m) -> q m", m=BLOCK))
+
         nc.scalar.activation(out=warm[:, 1:2], in_=warm[:, 0:1], func=ACT.Sigmoid)
 
         xt_ps = psum.tile([P, 2, 2, CELLS], F32)

@@ -39,7 +39,6 @@ def tile_fractalengine_pb_s_kernel(
     with ExitStack() as ctx:
         keep = ctx.enter_context(tc.tile_pool(name="keep", bufs=1))
         psum = ctx.enter_context(tc.psum_pool(name="psum", bufs=1))
-        ctx.enter_context(tc.manual_schedule())
 
         ident_f32 = keep.tile([P, P], F32)
         make_identity(nc, ident_f32[:])
@@ -56,14 +55,11 @@ def tile_fractalengine_pb_s_kernel(
         nc.sync.dma_start(out=x_sb[:, ENG, :], in_=eng_out)
         nc.sync.dma_start(out=x_sb[:, HIDDEN, :], in_=hiddens)
 
-        def load_scale_rows(quadrant):
+        for quadrant in range(4):
             nc.sync.dma_start(
                 out=whh_scales[32 * quadrant : 32 * quadrant + 4, :].bitcast(I32),
                 in_=w_hh_scales[0, 4 * quadrant : 4 * quadrant + 4, :].bitcast(I32),
             )
-
-        for quadrant in range(3):
-            load_scale_rows(quadrant)
 
         raw = {}
 
@@ -82,8 +78,6 @@ def tile_fractalengine_pb_s_kernel(
         nc.sync.dma_start(
             out=whh_words[:].bitcast(I32), in_=w_hh_words.rearrange("g p b -> (g p) b").bitcast(I32)
         )
-        load_columns(Z, (0, 1))
-        load_scale_rows(3)
         n_rows = GATES * BLOCKS
         tension_bc = keep.tile([P, CELLS], BF16)
         nc.scalar.dma_start(out=tension_bc[:], in_=tension.partition_broadcast(P))
@@ -91,11 +85,11 @@ def tile_fractalengine_pb_s_kernel(
             out=rows[2 * n_rows : 3 * n_rows, :],
             in_=w_ih[HID : HID + 1, :].rearrange("o (q m) -> (o q) m", m=BLOCK),
         )
+        nc.scalar.dma_start(out=rows[0:n_rows, :], in_=b_ih.rearrange("(q m) -> q m", m=BLOCK))
+        nc.scalar.dma_start(out=rows[n_rows : 2 * n_rows, :], in_=b_hh.rearrange("(q m) -> q m", m=BLOCK))
+        load_columns(Z, (0, 1))
         load_columns(N, (0,))
         load_columns(N, (1,))
-        nc.gpsimd.dma_start(out=rows[0:n_rows, :], in_=b_ih.rearrange("(q m) -> q m", m=BLOCK))
-        nc.gpsimd.dma_start(out=rows[n_rows : 2 * n_rows, :], in_=b_hh.rearrange("(q m) -> q m", m=BLOCK))
-
         nc.scalar.activation(out=warm[:, 1:2], in_=warm[:, 0:1], func=ACT.Sigmoid)
 
         xt_ps = psum.tile([P, 2, 2, CELLS], F32)

@@ -39,6 +39,7 @@ def tile_fractalengine_pb_s_kernel(
     with ExitStack() as ctx:
         keep = ctx.enter_context(tc.tile_pool(name="keep", bufs=1))
         psum = ctx.enter_context(tc.psum_pool(name="psum", bufs=1))
+        ctx.enter_context(tc.manual_schedule())
 
         ident_f32 = keep.tile([P, P], F32)
         make_identity(nc, ident_f32[:])
@@ -54,12 +55,15 @@ def tile_fractalengine_pb_s_kernel(
         x_sb = keep.tile([P, 2, HID], BF16)
         nc.sync.dma_start(out=x_sb[:, ENG, :], in_=eng_out)
         nc.sync.dma_start(out=x_sb[:, HIDDEN, :], in_=hiddens)
-
-        for quadrant in range(4):
-            nc.sync.dma_start(
-                out=whh_scales[32 * quadrant : 32 * quadrant + 4, :].bitcast(I32),
-                in_=w_hh_scales[0, 4 * quadrant : 4 * quadrant + 4, :].bitcast(I32),
-            )
+        n_rows = GATES * BLOCKS
+        tension_bc = keep.tile([P, CELLS], BF16)
+        nc.sync.dma_start(out=tension_bc[:], in_=tension.partition_broadcast(P))
+        nc.sync.dma_start(
+            out=rows[2 * n_rows : 3 * n_rows, :],
+            in_=w_ih[HID : HID + 1, :].rearrange("o (q m) -> (o q) m", m=BLOCK),
+        )
+        nc.sync.dma_start(out=rows[0:n_rows, :], in_=b_ih.rearrange("(q m) -> q m", m=BLOCK))
+        nc.sync.dma_start(out=rows[n_rows : 2 * n_rows, :], in_=b_hh.rearrange("(q m) -> q m", m=BLOCK))
 
         raw = {}
 
@@ -78,72 +82,63 @@ def tile_fractalengine_pb_s_kernel(
         nc.sync.dma_start(
             out=whh_words[:].bitcast(I32), in_=w_hh_words.rearrange("g p b -> (g p) b").bitcast(I32)
         )
-        n_rows = GATES * BLOCKS
-        tension_bc = keep.tile([P, CELLS], BF16)
-        nc.scalar.dma_start(out=tension_bc[:], in_=tension.partition_broadcast(P))
-        nc.scalar.dma_start(
-            out=rows[2 * n_rows : 3 * n_rows, :],
-            in_=w_ih[HID : HID + 1, :].rearrange("o (q m) -> (o q) m", m=BLOCK),
-        )
-        nc.scalar.dma_start(out=rows[0:n_rows, :], in_=b_ih.rearrange("(q m) -> q m", m=BLOCK))
-        nc.scalar.dma_start(out=rows[n_rows : 2 * n_rows, :], in_=b_hh.rearrange("(q m) -> q m", m=BLOCK))
+        for quadrant in range(4):
+            nc.sync.dma_start(
+                out=whh_scales[32 * quadrant : 32 * quadrant + 4, :].bitcast(I32),
+                in_=w_hh_scales[0, 4 * quadrant : 4 * quadrant + 4, :].bitcast(I32),
+            )
         load_columns(Z, (0, 1))
         load_columns(N, (0,))
         load_columns(N, (1,))
+
         nc.scalar.activation(out=warm[:, 1:2], in_=warm[:, 0:1], func=ACT.Sigmoid)
 
-        xt_ps = psum.tile([P, 2, 2, CELLS], F32)
-        x_words = x_sb[:].bitcast(F32)
-        for a in (ENG, HIDDEN):
-            for u in range(2):
-                nc.tensor.transpose(xt_ps[:, a, u, :], x_words[:, a, u : HID // 2 : 2], ident_f32[:])
-        x_grouped = keep.tile([P, 2, CELLS, PACK], BF16, align_bytes=64)
-        nc.scalar.copy(out=x_grouped[:].bitcast(F32), in_=xt_ps[:].rearrange("p a u c -> p a c u"))
-        x_codes = keep.tile([P, 2 * CELLS], U32, align_bytes=64)
-        x_scales = keep.tile([P, 2 * CELLS], U8, align_bytes=64)
-        nc.vector.quantize_mx(
-            out=x_codes[:].bitcast(FP8X4),
-            scales=x_scales[:],
-            in_=x_grouped[:].rearrange("p a c t -> p (a c t)"),
-        )
-
-        ht_ps = psum.tile([P, BLOCKS, CELLS], BF16)
-        for j in range(BLOCKS):
-            nc.tensor.transpose(ht_ps[:, j, :], x_sb[:, HIDDEN, j * BLOCK : (j + 1) * BLOCK], ident_bf16[:])
-        ht_sb = keep.tile([P, BLOCKS, CELLS], BF16)
-        nc.scalar.copy(out=ht_sb[:], in_=ht_ps[:])
-
+        whole = [P, BLOCKS, CELLS]
         rows_ps = psum.tile([P, P], BF16)
         cols = keep.tile([P, 3 * n_rows], F32)
-        minus_bias_z = keep.tile([P, BLOCKS], F32)
-        tension_n = keep.tile([P, BLOCKS, CELLS], F32)
+        table = keep.tile([P, n_rows, CELLS], F32)
 
         def small_vectors():
             nc.tensor.transpose(rows_ps[:], rows[:], ident_bf16[:])
             nc.vector.tensor_copy(out=cols[:], in_=rows_ps[:, 0 : 3 * n_rows])
             both = 2 * BLOCKS
             nc.vector.tensor_add(out=cols[:, 0:both], in0=cols[:, 0:both], in1=cols[:, n_rows : n_rows + both])
-            nc.vector.tensor_scalar_mul(
-                out=minus_bias_z[:], in0=cols[:, Z * BLOCKS : (Z + 1) * BLOCKS], scalar1=-1.0
-            )
-            for j in range(BLOCKS):
+            for q in range(n_rows):
                 nc.gpsimd.tensor_scalar(
-                    out=tension_n[:, j, :],
+                    out=table[:, q, :],
                     in0=tension_bc[:],
-                    scalar1=last_row(N, j),
-                    scalar2=bias(N, j),
+                    scalar1=cols[:, 2 * n_rows + q : 2 * n_rows + q + 1],
+                    scalar2=cols[:, q : q + 1],
                     op0=MULT,
                     op1=ADD,
                 )
 
-        def bias(g, j):
-            return cols[:, g * BLOCKS + j : g * BLOCKS + j + 1]
+        xt_ps = psum.tile([P, 2, 2, CELLS], F32)
+        x_grouped = keep.tile([P, 2, CELLS, PACK], BF16, align_bytes=64)
+        x_codes = keep.tile([P, 2 * CELLS], U32, align_bytes=64)
+        x_scales = keep.tile([P, 2 * CELLS], U8, align_bytes=64)
 
-        def bias_hn(j):
-            return cols[:, n_rows + N * BLOCKS + j : n_rows + N * BLOCKS + j + 1]
+        def transpose_activations():
+            x_words = x_sb[:].bitcast(F32)
+            for a in (ENG, HIDDEN):
+                for u in range(2):
+                    nc.tensor.transpose(xt_ps[:, a, u, :], x_words[:, a, u : HID // 2 : 2], ident_f32[:])
+            nc.scalar.copy(out=x_grouped[:].bitcast(F32), in_=xt_ps[:].rearrange("p a u c -> p a c u"))
 
-        def last_row(g, j):
-            return cols[:, 2 * n_rows + g * BLOCKS + j : 2 * n_rows + g * BLOCKS + j + 1]
+        def quantise_activations():
+            nc.vector.quantize_mx(
+                out=x_codes[:].bitcast(FP8X4),
+                scales=x_scales[:],
+                in_=x_grouped[:].rearrange("p a c t -> p (a c t)"),
+            )
+
+        ht_ps = psum.tile(whole, BF16)
+        ht_sb = keep.tile(whole, BF16)
+
+        def transpose_hiddens():
+            for j in range(BLOCKS):
+                nc.tensor.transpose(ht_ps[:, j, :], x_sb[:, HIDDEN, j * BLOCK : (j + 1) * BLOCK], ident_bf16[:])
+            nc.scalar.copy(out=ht_sb[:], in_=ht_ps[:])
 
         grouped = keep.tile([P, GATES * HID, PACK], BF16, align_bytes=64)
         wih_codes = keep.tile([P, GATES * HID], U32, align_bytes=64)
@@ -189,7 +184,6 @@ def tile_fractalengine_pb_s_kernel(
                 stop=stop,
             )
 
-        whole = [P, BLOCKS, CELLS]
         acc = [psum.tile(whole, F32, name="acc%d" % g) for g in (R, Z)]
         pre = [keep.tile(whole, F32, name="pre%d" % g) for g in (R, Z)]
         hn_ps = psum.tile(whole, F32)
@@ -224,22 +218,18 @@ def tile_fractalengine_pb_s_kernel(
             for b, j in enumerate(blocks_of(half)):
                 pass_ih(in_ps[half][:, b, :], N, j, True, True)
 
-        def add_tension(g):
-            for j in range(BLOCKS):
-                nc.vector.scalar_tensor_tensor(
-                    out=pre[g][:, j, :], in0=tension_bc[:], scalar=last_row(g, j), in1=acc[g][:, j, :], op0=MULT, op1=ADD
-                )
+        def add_table(g):
+            nc.vector.tensor_add(out=pre[g][:], in0=acc[g][:], in1=table[:, g * BLOCKS : (g + 1) * BLOCKS, :])
 
-        def sigmoid(dst, g, sign, biases):
-            for j in range(BLOCKS):
-                nc.scalar.activation(
-                    out=dst[:, j, :], in_=pre[g][:, j, :], func=ACT.Sigmoid, scale=sign, bias=biases[:, j : j + 1]
-                )
+        def sigmoid(dst, g, sign):
+            nc.scalar.activation(out=dst[:], in_=pre[g][:], func=ACT.Sigmoid, scale=sign)
+
+        bias_hn = n_rows + N * BLOCKS
 
         def r_times_hn():
             for j in range(BLOCKS):
                 nc.vector.scalar_tensor_tensor(
-                    out=rh[:, j, :], in0=hn_ps[:, j, :], scalar=bias_hn(j), in1=r[:, j, :], op0=ADD, op1=MULT
+                    out=rh[:, j, :], in0=hn_ps[:, j, :], scalar=cols[:, bias_hn + j : bias_hn + j + 1], in1=r[:, j, :], op0=ADD, op1=MULT
                 )
 
         def half_of(half):
@@ -247,7 +237,7 @@ def tile_fractalengine_pb_s_kernel(
 
         def rest_of_n(half):
             nc.gpsimd.tensor_add(
-                out=rest_n[:, half_of(half), :], in0=rh[:, half_of(half), :], in1=tension_n[:, half_of(half), :]
+                out=rest_n[:, half_of(half), :], in0=rh[:, half_of(half), :], in1=table[:, N * BLOCKS + half * HALF_BLOCKS : N * BLOCKS + (half + 1) * HALF_BLOCKS, :]
             )
 
         def z_times_h(half):
@@ -296,17 +286,20 @@ def tile_fractalengine_pb_s_kernel(
             nc.scalar.mul(out=out_sb[:, cols_of], in_=back_ps[:].rearrange("p b m -> p (b m)"), mul=1.0 - SYNC)
             nc.sync.dma_start(out=out[:, cols_of], in_=out_sb[:, cols_of])
 
+        transpose_activations()
+        small_vectors()
         regroup(R, 0)
         regroup(R, 1)
+        quantise_activations()
+        transpose_hiddens()
         quantise(R, 0)
         quantise(R, 1)
-        small_vectors()
         passes_hn()
         passes_both(R)
         regroup(Z, 0)
         regroup(Z, 1)
-        add_tension(R)
-        sigmoid(r, R, 1.0, cols[:, R * BLOCKS : (R + 1) * BLOCKS])
+        add_table(R)
+        sigmoid(r, R, 1.0)
         quantise(Z, 0)
         quantise(Z, 1)
         passes_both(Z)
@@ -315,11 +308,11 @@ def tile_fractalengine_pb_s_kernel(
         rest_of_n(1)
         regroup(N, 0)
         regroup(N, 1)
-        add_tension(Z)
-        sigmoid(z, Z, 1.0, cols[:, Z * BLOCKS : (Z + 1) * BLOCKS])
+        add_table(Z)
+        sigmoid(z, Z, 1.0)
         z_times_h(0)
         z_times_h(1)
-        sigmoid(one_minus_z, Z, -1.0, minus_bias_z)
+        sigmoid(one_minus_z, Z, -1.0)
         for half in range(HALVES):
             quantise(N, half)
             passes_in(half)

@@ -25,6 +25,7 @@ BLOCKS = HID // BLOCK
 FACTION = 16
 SYNC = 0.15
 ENG, HIDDEN = 0, 1
+TENSION_ROW = 64
 HALVES = 2
 HALF = HID // HALVES
 HALF_BLOCKS = HALF // BLOCK
@@ -47,6 +48,9 @@ def tile_fractalengine_pb_s_kernel(
         nc.vector.memset(whh_scales[:].bitcast(I32), 0)
         rows = keep.tile([P, P], BF16)
         nc.vector.memset(rows[:], 0.0)
+        pick = keep.tile([P, P], BF16)
+        nc.vector.memset(pick[:], 0.0)
+        nc.vector.memset(pick[TENSION_ROW : TENSION_ROW + 1, :], 1.0)
         warm = keep.tile([P, 2], F32)
         nc.vector.memset(warm[:], 0.0)
         ident_bf16 = keep.tile([P, P], BF16)
@@ -56,8 +60,7 @@ def tile_fractalengine_pb_s_kernel(
         nc.sync.dma_start(out=x_sb[:, ENG, :], in_=eng_out)
         nc.sync.dma_start(out=x_sb[:, HIDDEN, :], in_=hiddens)
         n_rows = GATES * BLOCKS
-        tension_bc = keep.tile([P, CELLS], BF16)
-        nc.sync.dma_start(out=tension_bc[:], in_=tension.partition_broadcast(P))
+        nc.sync.dma_start(out=rows[TENSION_ROW : TENSION_ROW + 1, :], in_=tension.rearrange("(o c) -> o c", o=1))
         nc.sync.dma_start(
             out=rows[2 * n_rows : 3 * n_rows, :],
             in_=w_ih[HID : HID + 1, :].rearrange("o (q m) -> (o q) m", m=BLOCK),
@@ -97,10 +100,14 @@ def tile_fractalengine_pb_s_kernel(
         rows_ps = psum.tile([P, P], BF16)
         cols = keep.tile([P, 3 * n_rows], F32)
         table = keep.tile([P, n_rows, CELLS], F32)
+        tension_ps = psum.tile([P, CELLS], F32, tag="in0")
+        tension_bc = keep.tile([P, CELLS], F32)
 
         def small_vectors():
             nc.tensor.transpose(rows_ps[:], rows[:], ident_bf16[:])
+            nc.tensor.matmul(out=tension_ps[:], lhsT=pick[:], rhs=rows[:], start=True, stop=True)
             nc.vector.tensor_copy(out=cols[:], in_=rows_ps[:, 0 : 3 * n_rows])
+            nc.vector.tensor_copy(out=tension_bc[:], in_=tension_ps[:])
             both = 2 * BLOCKS
             nc.vector.tensor_add(out=cols[:, 0:both], in0=cols[:, 0:both], in1=cols[:, n_rows : n_rows + both])
             for q in range(n_rows):

@@ -29,6 +29,9 @@ TENSION_ROW = 64
 HALVES = 2
 HALF = HID // HALVES
 HALF_BLOCKS = HALF // BLOCK
+VEC_ROWS = 4
+ROW = GATES * HID // VEC_ROWS
+ROW_BLOCKS = ROW // BLOCK
 
 FLOPS = 2 * CELLS * (HID + 1 + HID) * GATES * HID
 
@@ -44,10 +47,10 @@ def tile_fractalengine_pb_s_kernel(
 
         ident_f32 = keep.tile([P, P], F32)
         make_identity(nc, ident_f32[:])
+        rows = keep.tile([P, ROW], BF16)
+        nc.vector.memset(rows[:], 0.0)
         whh_scales = keep.tile([P, GATES * HID], U8, align_bytes=64)
         nc.vector.memset(whh_scales[:].bitcast(I32), 0)
-        rows = keep.tile([P, P], BF16)
-        nc.vector.memset(rows[:], 0.0)
         pick = keep.tile([P, P], BF16)
         nc.vector.memset(pick[:], 0.0)
         nc.vector.memset(pick[TENSION_ROW : TENSION_ROW + 1, :], 1.0)
@@ -60,13 +63,6 @@ def tile_fractalengine_pb_s_kernel(
         nc.sync.dma_start(out=x_sb[:, ENG, :], in_=eng_out)
         nc.sync.dma_start(out=x_sb[:, HIDDEN, :], in_=hiddens)
         n_rows = GATES * BLOCKS
-        nc.sync.dma_start(out=rows[TENSION_ROW : TENSION_ROW + 1, :], in_=tension.rearrange("(o c) -> o c", o=1))
-        nc.sync.dma_start(
-            out=rows[2 * n_rows : 3 * n_rows, :],
-            in_=w_ih[HID : HID + 1, :].rearrange("o (q m) -> (o q) m", m=BLOCK),
-        )
-        nc.sync.dma_start(out=rows[0:n_rows, :], in_=b_ih.rearrange("(q m) -> q m", m=BLOCK))
-        nc.sync.dma_start(out=rows[n_rows : 2 * n_rows, :], in_=b_hh.rearrange("(q m) -> q m", m=BLOCK))
 
         raw = {}
 
@@ -81,6 +77,14 @@ def tile_fractalengine_pb_s_kernel(
                 raw[(g, half)] = loaded[:, :, i * HALF : (i + 1) * HALF]
 
         load_columns(R, (0, 1))
+        nc.sync.dma_start(out=rows[TENSION_ROW : TENSION_ROW + 1, 0:CELLS], in_=tension.rearrange("(o c) -> o c", o=1))
+        nc.sync.dma_start(
+            out=rows[2 * VEC_ROWS : 3 * VEC_ROWS, :],
+            in_=w_ih[HID : HID + 1, :].rearrange("o (r m) -> (o r) m", m=ROW),
+        )
+        nc.sync.dma_start(out=rows[0:VEC_ROWS, :], in_=b_ih.rearrange("(r m) -> r m", m=ROW))
+        nc.sync.dma_start(out=rows[VEC_ROWS : 2 * VEC_ROWS, :], in_=b_hh.rearrange("(r m) -> r m", m=ROW))
+        load_columns(Z, (0, 1))
         whh_words = keep.tile([P, 2 * GATES * HID], U8, align_bytes=64)
         nc.sync.dma_start(
             out=whh_words[:].bitcast(I32), in_=w_hh_words.rearrange("g p b -> (g p) b").bitcast(I32)
@@ -90,23 +94,26 @@ def tile_fractalengine_pb_s_kernel(
                 out=whh_scales[32 * quadrant : 32 * quadrant + 4, :].bitcast(I32),
                 in_=w_hh_scales[0, 4 * quadrant : 4 * quadrant + 4, :].bitcast(I32),
             )
-        load_columns(Z, (0, 1))
         load_columns(N, (0,))
         load_columns(N, (1,))
 
         nc.scalar.activation(out=warm[:, 1:2], in_=warm[:, 0:1], func=ACT.Sigmoid)
 
         whole = [P, BLOCKS, CELLS]
-        rows_ps = psum.tile([P, P], BF16)
+        rows_ps = psum.tile([P, ROW_BLOCKS, P], BF16)
         cols = keep.tile([P, 3 * n_rows], F32)
         table = keep.tile([P, n_rows, CELLS], F32)
         tension_ps = psum.tile([P, CELLS], F32, tag="in0")
         tension_bc = keep.tile([P, CELLS], F32)
 
         def small_vectors():
-            nc.tensor.transpose(rows_ps[:], rows[:], ident_bf16[:])
-            nc.tensor.matmul(out=tension_ps[:], lhsT=pick[:], rhs=rows[:], start=True, stop=True)
-            nc.vector.tensor_copy(out=cols[:], in_=rows_ps[:, 0 : 3 * n_rows])
+            for c in range(ROW_BLOCKS):
+                nc.tensor.transpose(rows_ps[:, c, :], rows[:, c * BLOCK : (c + 1) * BLOCK], ident_bf16[:])
+            nc.tensor.matmul(out=tension_ps[:], lhsT=pick[:], rhs=rows[:, 0:CELLS], start=True, stop=True)
+            nc.vector.tensor_copy(
+                out=cols[:].rearrange("p (a c) -> p a c", c=ROW_BLOCKS),
+                in_=rows_ps[:, :, 0 : 3 * VEC_ROWS].rearrange("p c a -> p a c"),
+            )
             nc.vector.tensor_copy(out=tension_bc[:], in_=tension_ps[:])
             both = 2 * BLOCKS
             nc.vector.tensor_add(out=cols[:, 0:both], in0=cols[:, 0:both], in1=cols[:, n_rows : n_rows + both])
@@ -301,20 +308,20 @@ def tile_fractalengine_pb_s_kernel(
         transpose_hiddens()
         quantise(R, 0)
         quantise(R, 1)
-        passes_hn()
-        passes_both(R)
         regroup(Z, 0)
         regroup(Z, 1)
-        add_table(R)
-        sigmoid(r, R, 1.0)
         quantise(Z, 0)
         quantise(Z, 1)
+        passes_hn()
+        passes_both(R)
+        add_table(R)
+        sigmoid(r, R, 1.0)
         passes_both(Z)
+        regroup(N, 0)
+        regroup(N, 1)
         r_times_hn()
         rest_of_n(0)
         rest_of_n(1)
-        regroup(N, 0)
-        regroup(N, 1)
         add_table(Z)
         sigmoid(z, Z, 1.0)
         z_times_h(0)

@@ -32,6 +32,8 @@ HALF_BLOCKS = HALF // BLOCK
 VEC_ROWS = 4
 ROW = GATES * HID // VEC_ROWS
 ROW_BLOCKS = ROW // BLOCK
+N_COLS = GATES * BLOCKS
+B_IH, B_HH, W_LAST = 0, N_COLS, 2 * N_COLS
 
 FLOPS = 2 * CELLS * (HID + 1 + HID) * GATES * HID
 
@@ -60,11 +62,22 @@ def tile_fractalengine_pb_s_kernel(
         nc.vector.tensor_copy(out=ident_bf16[:], in_=ident_f32[:])
 
         x_sb = keep.tile([P, 2, HID], BF16)
-        nc.sync.dma_start(out=x_sb[:, ENG, :], in_=eng_out)
-        nc.sync.dma_start(out=x_sb[:, HIDDEN, :], in_=hiddens)
-        n_rows = GATES * BLOCKS
-
         raw = {}
+
+        def load_activations():
+            nc.sync.dma_start(out=x_sb[:, ENG, :], in_=eng_out)
+            nc.sync.dma_start(out=x_sb[:, HIDDEN, :], in_=hiddens)
+
+        def load_small_vectors():
+            nc.sync.dma_start(
+                out=rows[TENSION_ROW : TENSION_ROW + 1, 0:CELLS], in_=tension.rearrange("(o c) -> o c", o=1)
+            )
+            nc.sync.dma_start(
+                out=rows[2 * VEC_ROWS : 3 * VEC_ROWS, :],
+                in_=w_ih[HID : HID + 1, :].rearrange("o (r m) -> (o r) m", m=ROW),
+            )
+            nc.sync.dma_start(out=rows[0:VEC_ROWS, :], in_=b_ih.rearrange("(r m) -> r m", m=ROW))
+            nc.sync.dma_start(out=rows[VEC_ROWS : 2 * VEC_ROWS, :], in_=b_hh.rearrange("(r m) -> r m", m=ROW))
 
         def load_columns(g, halves):
             width = len(halves) * HALF
@@ -76,34 +89,46 @@ def tile_fractalengine_pb_s_kernel(
             for i, half in enumerate(halves):
                 raw[(g, half)] = loaded[:, :, i * HALF : (i + 1) * HALF]
 
-        load_columns(R, (0, 1))
-        nc.sync.dma_start(out=rows[TENSION_ROW : TENSION_ROW + 1, 0:CELLS], in_=tension.rearrange("(o c) -> o c", o=1))
-        nc.sync.dma_start(
-            out=rows[2 * VEC_ROWS : 3 * VEC_ROWS, :],
-            in_=w_ih[HID : HID + 1, :].rearrange("o (r m) -> (o r) m", m=ROW),
-        )
-        nc.sync.dma_start(out=rows[0:VEC_ROWS, :], in_=b_ih.rearrange("(r m) -> r m", m=ROW))
-        nc.sync.dma_start(out=rows[VEC_ROWS : 2 * VEC_ROWS, :], in_=b_hh.rearrange("(r m) -> r m", m=ROW))
-        load_columns(Z, (0, 1))
         whh_words = keep.tile([P, 2 * GATES * HID], U8, align_bytes=64)
-        nc.sync.dma_start(
-            out=whh_words[:].bitcast(I32), in_=w_hh_words.rearrange("g p b -> (g p) b").bitcast(I32)
-        )
-        for quadrant in range(4):
+
+        def load_whh():
             nc.sync.dma_start(
-                out=whh_scales[32 * quadrant : 32 * quadrant + 4, :].bitcast(I32),
-                in_=w_hh_scales[0, 4 * quadrant : 4 * quadrant + 4, :].bitcast(I32),
+                out=whh_words[:].bitcast(I32), in_=w_hh_words.rearrange("g p b -> (g p) b").bitcast(I32)
             )
+
+        def load_scales():
+            for quadrant in range(4):
+                nc.sync.dma_start(
+                    out=whh_scales[32 * quadrant : 32 * quadrant + 4, :].bitcast(I32),
+                    in_=w_hh_scales[0, 4 * quadrant : 4 * quadrant + 4, :].bitcast(I32),
+                )
+
+        load_activations()
+        load_columns(R, (0, 1))
+        load_small_vectors()
+        load_columns(Z, (0, 1))
+        load_whh()
+        load_scales()
         load_columns(N, (0,))
         load_columns(N, (1,))
 
         nc.scalar.activation(out=warm[:, 1:2], in_=warm[:, 0:1], func=ACT.Sigmoid)
 
         whole = [P, BLOCKS, CELLS]
-        rows_ps = psum.tile([P, ROW_BLOCKS, P], BF16)
-        cols = keep.tile([P, 3 * n_rows], F32)
-        table = keep.tile([P, n_rows, CELLS], F32)
-        tension_ps = psum.tile([P, CELLS], F32, tag="in0")
+        half_shape = [P, HALF_BLOCKS, CELLS]
+        xt_ps = psum.tile([P, 2, 2, CELLS], F32, tag="ra", name="xt_ps")
+        rows_ps = psum.tile([P, ROW_BLOCKS, P], BF16, tag="rb", name="rows_ps")
+        tension_ps = psum.tile([P, CELLS], F32, tag="za", name="tension_ps")
+        ht_ps = psum.tile(whole, BF16, tag="ht", name="ht_ps")
+        hn_ps = psum.tile(whole, F32, tag="hn", name="hn_ps")
+        acc = {
+            R: [psum.tile(half_shape, F32, tag="ra", name="acc_r0"), psum.tile(half_shape, F32, tag="rb", name="acc_r1")],
+            Z: [psum.tile(half_shape, F32, tag="za", name="acc_z0"), psum.tile(half_shape, F32, tag="zb", name="acc_z1")],
+        }
+        in_ps = [psum.tile(half_shape, F32, tag="ia", name="in_ps0"), psum.tile(half_shape, F32, tag="ib", name="in_ps1")]
+
+        cols = keep.tile([P, 3 * N_COLS], F32)
+        minus_bias_z = keep.tile([P, BLOCKS], F32)
         tension_bc = keep.tile([P, CELLS], F32)
 
         def small_vectors():
@@ -116,18 +141,11 @@ def tile_fractalengine_pb_s_kernel(
             )
             nc.vector.tensor_copy(out=tension_bc[:], in_=tension_ps[:])
             both = 2 * BLOCKS
-            nc.vector.tensor_add(out=cols[:, 0:both], in0=cols[:, 0:both], in1=cols[:, n_rows : n_rows + both])
-            for q in range(n_rows):
-                nc.gpsimd.tensor_scalar(
-                    out=table[:, q, :],
-                    in0=tension_bc[:],
-                    scalar1=cols[:, 2 * n_rows + q : 2 * n_rows + q + 1],
-                    scalar2=cols[:, q : q + 1],
-                    op0=MULT,
-                    op1=ADD,
-                )
+            nc.vector.tensor_add(out=cols[:, 0:both], in0=cols[:, 0:both], in1=cols[:, B_HH : B_HH + both])
 
-        xt_ps = psum.tile([P, 2, 2, CELLS], F32)
+        def negate_bias_z():
+            nc.vector.tensor_scalar_mul(out=minus_bias_z[:], in0=cols[:, Z * BLOCKS : (Z + 1) * BLOCKS], scalar1=-1.0)
+
         x_grouped = keep.tile([P, 2, CELLS, PACK], BF16, align_bytes=64)
         x_codes = keep.tile([P, 2 * CELLS], U32, align_bytes=64)
         x_scales = keep.tile([P, 2 * CELLS], U8, align_bytes=64)
@@ -146,22 +164,17 @@ def tile_fractalengine_pb_s_kernel(
                 in_=x_grouped[:].rearrange("p a c t -> p (a c t)"),
             )
 
-        ht_ps = psum.tile(whole, BF16)
-        ht_sb = keep.tile(whole, BF16)
-
         def transpose_hiddens():
             for j in range(BLOCKS):
                 nc.tensor.transpose(ht_ps[:, j, :], x_sb[:, HIDDEN, j * BLOCK : (j + 1) * BLOCK], ident_bf16[:])
-            nc.scalar.copy(out=ht_sb[:], in_=ht_ps[:])
 
         grouped = keep.tile([P, GATES * HID, PACK], BF16, align_bytes=64)
         wih_codes = keep.tile([P, GATES * HID], U32, align_bytes=64)
         wih_scales = keep.tile([P, GATES * HID], U8, align_bytes=64)
-        half_copy = (nc.vector.tensor_copy, nc.scalar.copy)
 
-        def regroup(g, half):
+        def regroup(copy, g, half):
             piece = slice(g * HID + half * HALF, g * HID + (half + 1) * HALF)
-            half_copy[half](
+            copy(
                 out=grouped[:, piece, :].rearrange("p (c i) t -> p c t i", i=4),
                 in_=raw[(g, half)].rearrange("p t (c i) -> p c t i", i=4),
             )
@@ -174,10 +187,10 @@ def tile_fractalengine_pb_s_kernel(
                 in_=grouped[:, piece, :].rearrange("p w t -> p (w t)"),
             )
 
-        def pass_hh(acc, g, j, start, stop):
+        def pass_hh(dst, g, j, start, stop):
             col = g * HID + j * BLOCK
             nc.tensor.matmul_mx(
-                out=acc,
+                out=dst,
                 lhsT=whh_words[:, 2 * col : 2 * (col + BLOCK)].bitcast(FP4X4),
                 lhsT_scale=whh_scales[:, col : col + BLOCK],
                 rhs=x_codes[:, CELLS : 2 * CELLS].bitcast(FP8X4),
@@ -186,10 +199,10 @@ def tile_fractalengine_pb_s_kernel(
                 stop=stop,
             )
 
-        def pass_ih(acc, g, j, start, stop):
+        def pass_ih(dst, g, j, start, stop):
             col = g * HID + j * BLOCK
             nc.tensor.matmul_mx(
-                out=acc,
+                out=dst,
                 lhsT=wih_codes[:, col : col + BLOCK].bitcast(FP8X4),
                 lhsT_scale=wih_scales[:, col : col + BLOCK],
                 rhs=x_codes[:, 0:CELLS].bitcast(FP8X4),
@@ -198,10 +211,7 @@ def tile_fractalengine_pb_s_kernel(
                 stop=stop,
             )
 
-        acc = [psum.tile(whole, F32, name="acc%d" % g) for g in (R, Z)]
-        pre = [keep.tile(whole, F32, name="pre%d" % g) for g in (R, Z)]
-        hn_ps = psum.tile(whole, F32)
-        in_ps = [psum.tile([P, HALF_BLOCKS, CELLS], F32, name="in%d" % half) for half in range(HALVES)]
+        pre = {g: keep.tile(whole, F32, name="pre%d" % g) for g in (R, Z)}
         r = keep.tile(whole, F32)
         rh = keep.tile(whole, F32)
         rest_n = keep.tile(whole, F32)
@@ -219,47 +229,61 @@ def tile_fractalengine_pb_s_kernel(
         def blocks_of(half):
             return range(half * HALF_BLOCKS, (half + 1) * HALF_BLOCKS)
 
+        def half_of(half):
+            return slice(half * HALF_BLOCKS, (half + 1) * HALF_BLOCKS)
+
+        def column(first, g, j):
+            k = first + g * BLOCKS + j
+            return cols[:, k : k + 1]
+
         def passes_hn():
             for j in range(BLOCKS):
                 pass_hh(hn_ps[:, j, :], N, j, True, True)
 
-        def passes_both(g):
-            for j in range(BLOCKS):
-                pass_hh(acc[g][:, j, :], g, j, True, False)
-                pass_ih(acc[g][:, j, :], g, j, False, True)
+        def passes_both(g, half):
+            for b, j in enumerate(blocks_of(half)):
+                pass_hh(acc[g][half][:, b, :], g, j, True, False)
+                pass_ih(acc[g][half][:, b, :], g, j, False, True)
 
         def passes_in(half):
             for b, j in enumerate(blocks_of(half)):
                 pass_ih(in_ps[half][:, b, :], N, j, True, True)
 
-        def add_table(g):
-            nc.vector.tensor_add(out=pre[g][:], in0=acc[g][:], in1=table[:, g * BLOCKS : (g + 1) * BLOCKS, :])
+        def add_tension(g, j):
+            nc.vector.scalar_tensor_tensor(
+                out=pre[g][:, j, :], in0=tension_bc[:], scalar=column(W_LAST, g, j),
+                in1=acc[g][j // HALF_BLOCKS][:, j % HALF_BLOCKS, :], op0=MULT, op1=ADD,
+            )
 
-        def sigmoid(dst, g, sign):
-            nc.scalar.activation(out=dst[:], in_=pre[g][:], func=ACT.Sigmoid, scale=sign)
+        def gate_r(j):
+            nc.scalar.activation(out=r[:, j, :], in_=pre[R][:, j, :], func=ACT.Sigmoid, bias=column(B_IH, R, j))
 
-        bias_hn = n_rows + N * BLOCKS
+        def gate_z(j):
+            nc.scalar.activation(out=z[:, j, :], in_=pre[Z][:, j, :], func=ACT.Sigmoid, bias=column(B_IH, Z, j))
 
-        def r_times_hn():
-            for j in range(BLOCKS):
-                nc.vector.scalar_tensor_tensor(
-                    out=rh[:, j, :], in0=hn_ps[:, j, :], scalar=cols[:, bias_hn + j : bias_hn + j + 1], in1=r[:, j, :], op0=ADD, op1=MULT
-                )
+        def gate_one_minus_z(j):
+            nc.scalar.activation(
+                out=one_minus_z[:, j, :], in_=pre[Z][:, j, :], func=ACT.Sigmoid, scale=-1.0, bias=minus_bias_z[:, j : j + 1]
+            )
 
-        def half_of(half):
-            return slice(half * HALF_BLOCKS, (half + 1) * HALF_BLOCKS)
+        def r_times_hn(j):
+            nc.vector.scalar_tensor_tensor(
+                out=rh[:, j, :], in0=hn_ps[:, j, :], scalar=column(B_HH, N, j), in1=r[:, j, :], op0=ADD, op1=MULT
+            )
 
-        def rest_of_n(half):
-            nc.gpsimd.tensor_add(
-                out=rest_n[:, half_of(half), :], in0=rh[:, half_of(half), :], in1=table[:, N * BLOCKS + half * HALF_BLOCKS : N * BLOCKS + (half + 1) * HALF_BLOCKS, :]
+        def rest_of_n(j):
+            nc.vector.scalar_tensor_tensor(
+                out=rest_n[:, j, :], in0=tension_bc[:], scalar=column(W_LAST, N, j), in1=rh[:, j, :], op0=MULT, op1=ADD
             )
 
         def z_times_h(half):
-            nc.gpsimd.tensor_mul(out=zh[:, half_of(half), :], in0=z[:, half_of(half), :], in1=ht_sb[:, half_of(half), :])
+            nc.vector.tensor_mul(out=zh[:, half_of(half), :], in0=z[:, half_of(half), :], in1=ht_ps[:, half_of(half), :])
 
-        def candidate(half):
+        def argument_of_n(half):
             nc.vector.tensor_add(out=pre_n[:, half_of(half), :], in0=in_ps[half][:], in1=rest_n[:, half_of(half), :])
-            nc.scalar.activation(out=n_cand[:, half_of(half), :], in_=pre_n[:, half_of(half), :], func=ACT.Tanh)
+
+        def candidate(j):
+            nc.scalar.activation(out=n_cand[:, j, :], in_=pre_n[:, j, :], func=ACT.Tanh, bias=column(B_IH, N, j))
 
         def keep_fresh(half):
             nc.vector.tensor_mul(
@@ -292,52 +316,66 @@ def tile_fractalengine_pb_s_kernel(
                 op1=ADD,
             )
 
-        def store(half):
+        def store(half, bank):
             cols_of = slice(half * HALF, (half + 1) * HALF)
-            back_ps = psum.tile([P, HALF_BLOCKS, BLOCK], F32, tag="acc%d" % half, name="back%d" % half)
+            back_ps = psum.tile([P, HALF_BLOCKS, BLOCK], F32, tag=bank, name="back%d" % half)
             for b, j in enumerate(blocks_of(half)):
                 nc.tensor.transpose(back_ps[:, b, :], mixed[:, j, :], ident_f32[:])
             nc.scalar.mul(out=out_sb[:, cols_of], in_=back_ps[:].rearrange("p b m -> p (b m)"), mul=1.0 - SYNC)
             nc.sync.dma_start(out=out[:, cols_of], in_=out_sb[:, cols_of])
 
+        by_vector = nc.vector.tensor_copy
+        by_scalar = nc.scalar.copy
+
         transpose_activations()
+        regroup(by_vector, R, 0)
+        regroup(by_scalar, R, 1)
         small_vectors()
-        regroup(R, 0)
-        regroup(R, 1)
         quantise_activations()
         transpose_hiddens()
         quantise(R, 0)
         quantise(R, 1)
-        regroup(Z, 0)
-        regroup(Z, 1)
+        regroup(by_vector, Z, 0)
+        regroup(by_scalar, Z, 1)
+        negate_bias_z()
         quantise(Z, 0)
         quantise(Z, 1)
+        passes_both(R, 0)
+        passes_both(R, 1)
         passes_hn()
-        passes_both(R)
-        add_table(R)
-        sigmoid(r, R, 1.0)
-        passes_both(Z)
-        regroup(N, 0)
-        regroup(N, 1)
-        r_times_hn()
-        rest_of_n(0)
-        rest_of_n(1)
-        add_table(Z)
-        sigmoid(z, Z, 1.0)
-        z_times_h(0)
-        z_times_h(1)
-        sigmoid(one_minus_z, Z, -1.0)
-        for half in range(HALVES):
-            quantise(N, half)
-            passes_in(half)
-        for half in range(HALVES):
-            candidate(half)
-        for half in range(HALVES):
+        passes_both(Z, 0)
+        passes_both(Z, 1)
+        for j in range(BLOCKS):
+            add_tension(R, j)
+            gate_r(j)
+        regroup(by_vector, N, 1)
+        regroup(by_scalar, N, 0)
+        for j in range(BLOCKS):
+            r_times_hn(j)
+        for j in range(BLOCKS):
+            rest_of_n(j)
+        quantise(N, 1)
+        passes_in(1)
+        for j in range(BLOCKS):
+            add_tension(Z, j)
+            gate_z(j)
+        quantise(N, 0)
+        passes_in(0)
+        for j in range(BLOCKS):
+            gate_one_minus_z(j)
+        order = (1, 0)
+        for half in order:
+            argument_of_n(half)
+            for j in blocks_of(half):
+                candidate(j)
+        for half in order:
+            z_times_h(half)
+        for half in order:
             keep_fresh(half)
-        for half in range(HALVES):
+        for half in order:
             new_state(half)
-        for half in range(HALVES):
+        for half in order:
             faction_sums(half)
-        for half in range(HALVES):
+        for half, bank in zip(order, ("ra", "rb")):
             pull(half)
-            store(half)
+            store(half, bank)

@@ -271,9 +271,16 @@ def tile_fractalengine_pb_s_kernel(
                 out=rh[:, j, :], in0=hn_ps[:, j, :], scalar=column(B_HH, N, j), in1=r[:, j, :], op0=ADD, op1=MULT
             )
 
-        def rest_of_n(j):
-            nc.vector.scalar_tensor_tensor(
-                out=rest_n[:, j, :], in0=tension_bc[:], scalar=column(W_LAST, N, j), in1=rh[:, j, :], op0=MULT, op1=ADD
+        table_n = keep.tile(whole, F32)
+
+        def tension_term_of_n(j):
+            nc.scalar.activation(
+                out=table_n[:, j, :], in_=tension_bc[:], func=ACT.Identity, scale=column(W_LAST, N, j), bias=column(B_IH, N, j)
+            )
+
+        def rest_of_n(half):
+            nc.gpsimd.tensor_add(
+                out=rest_n[:, half_of(half), :], in0=rh[:, half_of(half), :], in1=table_n[:, half_of(half), :]
             )
 
         def z_times_h(half):
@@ -282,8 +289,8 @@ def tile_fractalengine_pb_s_kernel(
         def argument_of_n(half):
             nc.vector.tensor_add(out=pre_n[:, half_of(half), :], in0=in_ps[half][:], in1=rest_n[:, half_of(half), :])
 
-        def candidate(j):
-            nc.scalar.activation(out=n_cand[:, j, :], in_=pre_n[:, j, :], func=ACT.Tanh, bias=column(B_IH, N, j))
+        def candidate(half):
+            nc.scalar.activation(out=n_cand[:, half_of(half), :], in_=pre_n[:, half_of(half), :], func=ACT.Tanh)
 
         def keep_fresh(half):
             nc.vector.tensor_mul(
@@ -346,19 +353,21 @@ def tile_fractalengine_pb_s_kernel(
         passes_both(Z, 0)
         passes_both(Z, 1)
         for j in range(BLOCKS):
+            tension_term_of_n(j)
+        for j in range(BLOCKS):
             add_tension(R, j)
             gate_r(j)
         regroup(by_vector, N, 1)
         regroup(by_scalar, N, 0)
-        for j in range(BLOCKS):
-            r_times_hn(j)
-        for j in range(BLOCKS):
-            rest_of_n(j)
-        quantise(N, 1)
-        passes_in(1)
+        for half in range(HALVES):
+            for j in blocks_of(half):
+                r_times_hn(j)
+            rest_of_n(half)
         for j in range(BLOCKS):
             add_tension(Z, j)
             gate_z(j)
+        quantise(N, 1)
+        passes_in(1)
         quantise(N, 0)
         passes_in(0)
         for j in range(BLOCKS):
@@ -366,8 +375,7 @@ def tile_fractalengine_pb_s_kernel(
         order = (1, 0)
         for half in order:
             argument_of_n(half)
-            for j in blocks_of(half):
-                candidate(j)
+            candidate(half)
         for half in order:
             z_times_h(half)
         for half in order:

@@ -97,10 +97,10 @@ def tile_fractalengine_pb_s_kernel(
             )
 
         def load_scales():
-            for quadrant in range(4):
+            for row in range(4):
                 nc.sync.dma_start(
-                    out=whh_scales[32 * quadrant : 32 * quadrant + 4, :].bitcast(I32),
-                    in_=w_hh_scales[0, 4 * quadrant : 4 * quadrant + 4, :].bitcast(I32),
+                    out=whh_scales[row:P:32, :].bitcast(I32),
+                    in_=w_hh_scales[0, row:16:4, :].bitcast(I32),
                 )
 
         load_activations()
@@ -109,8 +109,7 @@ def tile_fractalengine_pb_s_kernel(
         load_columns(Z, (0, 1))
         load_whh()
         load_scales()
-        load_columns(N, (0,))
-        load_columns(N, (1,))
+        load_columns(N, (0, 1))
 
         nc.scalar.activation(out=warm[:, 1:2], in_=warm[:, 0:1], func=ACT.Sigmoid)
 

@@ -127,7 +127,6 @@ def tile_fractalengine_pb_s_kernel(
         in_ps = [psum.tile(half_shape, F32, tag="ia", name="in_ps0"), psum.tile(half_shape, F32, tag="ib", name="in_ps1")]
 
         cols = keep.tile([P, 3 * N_COLS], F32)
-        minus_bias_z = keep.tile([P, BLOCKS], F32)
         tension_bc = keep.tile([P, CELLS], F32)
 
         def small_vectors():
@@ -141,9 +140,6 @@ def tile_fractalengine_pb_s_kernel(
             nc.vector.tensor_copy(out=tension_bc[:], in_=tension_ps[:])
             both = 2 * BLOCKS
             nc.vector.tensor_add(out=cols[:, 0:both], in0=cols[:, 0:both], in1=cols[:, B_HH : B_HH + both])
-
-        def negate_bias_z():
-            nc.vector.tensor_scalar_mul(out=minus_bias_z[:], in0=cols[:, Z * BLOCKS : (Z + 1) * BLOCKS], scalar1=-1.0)
 
         x_grouped = keep.tile([P, 2, CELLS, PACK], BF16, align_bytes=64)
         x_codes = keep.tile([P, 2 * CELLS], U32, align_bytes=64)
@@ -260,9 +256,9 @@ def tile_fractalengine_pb_s_kernel(
         def gate_z(j):
             nc.scalar.activation(out=z[:, j, :], in_=pre[Z][:, j, :], func=ACT.Sigmoid, bias=column(B_IH, Z, j))
 
-        def gate_one_minus_z(j):
-            nc.scalar.activation(
-                out=one_minus_z[:, j, :], in_=pre[Z][:, j, :], func=ACT.Sigmoid, scale=-1.0, bias=minus_bias_z[:, j : j + 1]
+        def gate_one_minus_z(half):
+            nc.gpsimd.tensor_scalar(
+                out=one_minus_z[:, half_of(half), :], in0=z[:, half_of(half), :], scalar1=-1.0, scalar2=1.0, op0=MULT, op1=ADD
             )
 
         def r_times_hn(j):
@@ -343,7 +339,6 @@ def tile_fractalengine_pb_s_kernel(
         quantise(R, 1)
         regroup(by_vector, Z, 0)
         regroup(by_scalar, Z, 1)
-        negate_bias_z()
         quantise(Z, 0)
         quantise(Z, 1)
         passes_both(R, 0)
@@ -369,9 +364,9 @@ def tile_fractalengine_pb_s_kernel(
         passes_in(1)
         quantise(N, 0)
         passes_in(0)
-        for j in range(BLOCKS):
-            gate_one_minus_z(j)
         order = (1, 0)
+        for half in order:
+            gate_one_minus_z(half)
         for half in order:
             argument_of_n(half)
             candidate(half)

from contextlib import ExitStack

import concourse.mybir as mybir
from concourse.masks import make_identity

F32 = mybir.dt.float32
BF16 = mybir.dt.bfloat16
I32 = mybir.dt.int32
U32 = mybir.dt.uint32
U8 = mybir.dt.uint8
FP8X4 = mybir.dt.float8_e4m3fn_x4
FP4X4 = mybir.dt.float4_e2m1fn_x4
ADD = mybir.AluOpType.add
MULT = mybir.AluOpType.mult
ACT = mybir.ActivationFunctionType

P = 128
PACK = 4
CELLS = 128
HID = 512
GATES = 3
R, Z, N = 0, 1, 2
BLOCK = 128
BLOCKS = HID // BLOCK
FACTION = 16
SYNC = 0.15
ENG, HIDDEN = 0, 1
TENSION_ROW = 64
HALVES = 2
HALF = HID // HALVES
HALF_BLOCKS = HALF // BLOCK
VEC_ROWS = 4
ROW = GATES * HID // VEC_ROWS
ROW_BLOCKS = ROW // BLOCK
N_COLS = GATES * BLOCKS
B_IH, B_HH, W_LAST = 0, N_COLS, 2 * N_COLS

FLOPS = 2 * CELLS * (HID + 1 + HID) * GATES * HID


def tile_fractalengine_pb_s_kernel(
    tc, eng_out, tension, hiddens, w_ih, b_ih, w_hh_words, w_hh_scales, b_hh, out
):
    nc = tc.nc
    with ExitStack() as ctx:
        keep = ctx.enter_context(tc.tile_pool(name="keep", bufs=1))
        psum = ctx.enter_context(tc.psum_pool(name="psum", bufs=1))
        ctx.enter_context(tc.manual_schedule())

        ident_f32 = keep.tile([P, P], F32)
        make_identity(nc, ident_f32[:])
        rows = keep.tile([P, ROW], BF16)
        nc.vector.memset(rows[:], 0.0)
        whh_scales = keep.tile([P, GATES * HID], U8, align_bytes=64)
        nc.vector.memset(whh_scales[:].bitcast(I32), 0)
        pick = keep.tile([P, P], BF16)
        nc.vector.memset(pick[:], 0.0)
        nc.vector.memset(pick[TENSION_ROW : TENSION_ROW + 1, :], 1.0)
        warm = keep.tile([P, 2], F32)
        nc.vector.memset(warm[:], 0.0)
        ident_bf16 = keep.tile([P, P], BF16)
        nc.vector.tensor_copy(out=ident_bf16[:], in_=ident_f32[:])

        x_sb = keep.tile([P, 2, HID], BF16)
        raw = {}

        def load_activations():
            nc.sync.dma_start(out=x_sb[:, ENG, :], in_=eng_out)
            nc.sync.dma_start(out=x_sb[:, HIDDEN, :], in_=hiddens)

        def load_small_vectors():
            nc.sync.dma_start(
                out=rows[TENSION_ROW : TENSION_ROW + 1, 0:CELLS], in_=tension.rearrange("(o c) -> o c", o=1)
            )
            nc.sync.dma_start(
                out=rows[2 * VEC_ROWS : 3 * VEC_ROWS, :],
                in_=w_ih[HID : HID + 1, :].rearrange("o (r m) -> (o r) m", m=ROW),
            )
            nc.sync.dma_start(out=rows[0:VEC_ROWS, :], in_=b_ih.rearrange("(r m) -> r m", m=ROW))
            nc.sync.dma_start(out=rows[VEC_ROWS : 2 * VEC_ROWS, :], in_=b_hh.rearrange("(r m) -> r m", m=ROW))

        def load_columns(g, halves):
            width = len(halves) * HALF
            first = g * HID + halves[0] * HALF
            loaded = keep.tile([P, PACK, width], BF16, name="raw%d%d" % (g, halves[0]))
            nc.sync.dma_start(
                out=loaded[:], in_=w_ih[0:HID, first : first + width].rearrange("(p t) w -> p t w", t=PACK)
            )
            for i, half in enumerate(halves):
                raw[(g, half)] = loaded[:, :, i * HALF : (i + 1) * HALF]

        whh_words = keep.tile([P, 2 * GATES * HID], U8, align_bytes=64)

        def load_whh():
            nc.sync.dma_start(
                out=whh_words[:].bitcast(I32), in_=w_hh_words.rearrange("g p b -> (g p) b").bitcast(I32)
            )

        def load_scales():
            for row in range(4):
                nc.sync.dma_start(
                    out=whh_scales[row:P:32, :].bitcast(I32),
                    in_=w_hh_scales[0, row:16:4, :].bitcast(I32),
                )

        load_activations()
        load_columns(R, (0, 1))
        load_small_vectors()
        load_columns(Z, (0, 1))
        load_whh()
        load_scales()
        load_columns(N, (0, 1))

        nc.scalar.activation(out=warm[:, 1:2], in_=warm[:, 0:1], func=ACT.Sigmoid)

        whole = [P, BLOCKS, CELLS]
        half_shape = [P, HALF_BLOCKS, CELLS]
        xt_ps = psum.tile([P, 2, 2, CELLS], F32, tag="ra", name="xt_ps")
        rows_ps = psum.tile([P, ROW_BLOCKS, P], BF16, tag="rb", name="rows_ps")
        tension_ps = psum.tile([P, CELLS], F32, tag="za", name="tension_ps")
        ht_ps = psum.tile(whole, BF16, tag="ht", name="ht_ps")
        hn_ps = psum.tile(whole, F32, tag="hn", name="hn_ps")
        acc = {
            R: [psum.tile(half_shape, F32, tag="ra", name="acc_r0"), psum.tile(half_shape, F32, tag="rb", name="acc_r1")],
            Z: [psum.tile(half_shape, F32, tag="za", name="acc_z0"), psum.tile(half_shape, F32, tag="zb", name="acc_z1")],
        }
        in_ps = [psum.tile(half_shape, F32, tag="ia", name="in_ps0"), psum.tile(half_shape, F32, tag="ib", name="in_ps1")]

        cols = keep.tile([P, 3 * N_COLS], F32)
        tension_bc = keep.tile([P, CELLS], F32)

        def small_vectors():
            for c in range(ROW_BLOCKS):
                nc.tensor.transpose(rows_ps[:, c, :], rows[:, c * BLOCK : (c + 1) * BLOCK], ident_bf16[:])
            nc.tensor.matmul(out=tension_ps[:], lhsT=pick[:], rhs=rows[:, 0:CELLS], start=True, stop=True)
            nc.vector.tensor_copy(
                out=cols[:].rearrange("p (a c) -> p a c", c=ROW_BLOCKS),
                in_=rows_ps[:, :, 0 : 3 * VEC_ROWS].rearrange("p c a -> p a c"),
            )
            nc.vector.tensor_copy(out=tension_bc[:], in_=tension_ps[:])
            both = 2 * BLOCKS
            nc.vector.tensor_add(out=cols[:, 0:both], in0=cols[:, 0:both], in1=cols[:, B_HH : B_HH + both])

        x_grouped = keep.tile([P, 2, CELLS, PACK], BF16, align_bytes=64)
        x_codes = keep.tile([P, 2 * CELLS], U32, align_bytes=64)
        x_scales = keep.tile([P, 2 * CELLS], U8, align_bytes=64)

        def transpose_activations():
            x_words = x_sb[:].bitcast(F32)
            for a in (ENG, HIDDEN):
                for u in range(2):
                    nc.tensor.transpose(xt_ps[:, a, u, :], x_words[:, a, u : HID // 2 : 2], ident_f32[:])
            nc.scalar.copy(out=x_grouped[:].bitcast(F32), in_=xt_ps[:].rearrange("p a u c -> p a c u"))

        def quantise_activations():
            nc.vector.quantize_mx(
                out=x_codes[:].bitcast(FP8X4),
                scales=x_scales[:],
                in_=x_grouped[:].rearrange("p a c t -> p (a c t)"),
            )

        def transpose_hiddens():
            for j in range(BLOCKS):
                nc.tensor.transpose(ht_ps[:, j, :], x_sb[:, HIDDEN, j * BLOCK : (j + 1) * BLOCK], ident_bf16[:])

        grouped = keep.tile([P, GATES * HID, PACK], BF16, align_bytes=64)
        wih_codes = keep.tile([P, GATES * HID], U32, align_bytes=64)
        wih_scales = keep.tile([P, GATES * HID], U8, align_bytes=64)

        def regroup(copy, g, half):
            piece = slice(g * HID + half * HALF, g * HID + (half + 1) * HALF)
            copy(
                out=grouped[:, piece, :].rearrange("p (c i) t -> p c t i", i=4),
                in_=raw[(g, half)].rearrange("p t (c i) -> p c t i", i=4),
            )

        def quantise(g, half):
            piece = slice(g * HID + half * HALF, g * HID + (half + 1) * HALF)
            nc.vector.quantize_mx(
                out=wih_codes[:, piece].bitcast(FP8X4),
                scales=wih_scales[:, piece],
                in_=grouped[:, piece, :].rearrange("p w t -> p (w t)"),
            )

        def pass_hh(dst, g, j, start, stop):
            col = g * HID + j * BLOCK
            nc.tensor.matmul_mx(
                out=dst,
                lhsT=whh_words[:, 2 * col : 2 * (col + BLOCK)].bitcast(FP4X4),
                lhsT_scale=whh_scales[:, col : col + BLOCK],
                rhs=x_codes[:, CELLS : 2 * CELLS].bitcast(FP8X4),
                rhs_scale=x_scales[:, CELLS : 2 * CELLS],
                start=start,
                stop=stop,
            )

        def pass_ih(dst, g, j, start, stop):
            col = g * HID + j * BLOCK
            nc.tensor.matmul_mx(
                out=dst,
                lhsT=wih_codes[:, col : col + BLOCK].bitcast(FP8X4),
                lhsT_scale=wih_scales[:, col : col + BLOCK],
                rhs=x_codes[:, 0:CELLS].bitcast(FP8X4),
                rhs_scale=x_scales[:, 0:CELLS],
                start=start,
                stop=stop,
            )

        pre = {g: keep.tile(whole, F32, name="pre%d" % g) for g in (R, Z)}
        r = keep.tile(whole, F32)
        rh = keep.tile(whole, F32)
        rest_n = keep.tile(whole, F32)
        z = keep.tile(whole, F32)
        one_minus_z = keep.tile(whole, F32)
        zh = keep.tile(whole, F32)
        pre_n = keep.tile(whole, F32)
        n_cand = keep.tile(whole, F32)
        fresh = keep.tile(whole, F32)
        h_new = keep.tile(whole, F32)
        mixed = keep.tile(whole, F32)
        fsum = keep.tile([P, BLOCKS * CELLS // FACTION], F32)
        out_sb = keep.tile([P, HID], F32)

        def blocks_of(half):
            return range(half * HALF_BLOCKS, (half + 1) * HALF_BLOCKS)

        def half_of(half):
            return slice(half * HALF_BLOCKS, (half + 1) * HALF_BLOCKS)

        def column(first, g, j):
            k = first + g * BLOCKS + j
            return cols[:, k : k + 1]

        def passes_hn():
            for j in range(BLOCKS):
                pass_hh(hn_ps[:, j, :], N, j, True, True)

        def passes_both(g, half):
            for b, j in enumerate(blocks_of(half)):
                pass_hh(acc[g][half][:, b, :], g, j, True, False)
                pass_ih(acc[g][half][:, b, :], g, j, False, True)

        def passes_in(half):
            for b, j in enumerate(blocks_of(half)):
                pass_ih(in_ps[half][:, b, :], N, j, True, True)

        def add_tension(g, j):
            nc.vector.scalar_tensor_tensor(
                out=pre[g][:, j, :], in0=tension_bc[:], scalar=column(W_LAST, g, j),
                in1=acc[g][j // HALF_BLOCKS][:, j % HALF_BLOCKS, :], op0=MULT, op1=ADD,
            )

        def gate_r(j):
            nc.scalar.activation(out=r[:, j, :], in_=pre[R][:, j, :], func=ACT.Sigmoid, bias=column(B_IH, R, j))

        def gate_z(j):
            nc.scalar.activation(out=z[:, j, :], in_=pre[Z][:, j, :], func=ACT.Sigmoid, bias=column(B_IH, Z, j))

        def gate_one_minus_z(half):
            nc.gpsimd.tensor_scalar(
                out=one_minus_z[:, half_of(half), :], in0=z[:, half_of(half), :], scalar1=-1.0, scalar2=1.0, op0=MULT, op1=ADD
            )

        def r_times_hn(j):
            nc.vector.scalar_tensor_tensor(
                out=rh[:, j, :], in0=hn_ps[:, j, :], scalar=column(B_HH, N, j), in1=r[:, j, :], op0=ADD, op1=MULT
            )

        table_n = keep.tile(whole, F32)

        def tension_term_of_n(j):
            nc.scalar.activation(
                out=table_n[:, j, :], in_=tension_bc[:], func=ACT.Identity, scale=column(W_LAST, N, j), bias=column(B_IH, N, j)
            )

        def rest_of_n(half):
            nc.gpsimd.tensor_add(
                out=rest_n[:, half_of(half), :], in0=rh[:, half_of(half), :], in1=table_n[:, half_of(half), :]
            )

        def z_times_h(half):
            nc.vector.tensor_mul(out=zh[:, half_of(half), :], in0=z[:, half_of(half), :], in1=ht_ps[:, half_of(half), :])

        def argument_of_n(half):
            nc.vector.tensor_add(out=pre_n[:, half_of(half), :], in0=in_ps[half][:], in1=rest_n[:, half_of(half), :])

        def candidate(half):
            nc.scalar.activation(out=n_cand[:, half_of(half), :], in_=pre_n[:, half_of(half), :], func=ACT.Tanh)

        def keep_fresh(half):
            nc.vector.tensor_mul(
                out=fresh[:, half_of(half), :], in0=one_minus_z[:, half_of(half), :], in1=n_cand[:, half_of(half), :]
            )

        def new_state(half):
            nc.vector.tensor_add(
                out=h_new[:, half_of(half), :], in0=fresh[:, half_of(half), :], in1=zh[:, half_of(half), :]
            )

        by_faction = "p b (f i) -> p (b f) i"
        factions = HALF_BLOCKS * CELLS // FACTION

        def faction_sums(half):
            nc.vector.tensor_reduce(
                out=fsum[:, half * factions : (half + 1) * factions],
                in_=h_new[:, half_of(half), :].rearrange(by_faction, i=FACTION),
                axis=mybir.AxisListType.X,
                op=ADD,
            )

        def pull(half):
            nc.vector.scalar_tensor_tensor(
                out=mixed[:, half_of(half), :].rearrange(by_faction, i=FACTION),
                in0=fsum[:, half * factions : (half + 1) * factions].unsqueeze(2).to_broadcast([P, factions, FACTION]),
                scalar=SYNC / (1.0 - SYNC) / FACTION,
                in1=h_new[:, half_of(half), :].rearrange(by_faction, i=FACTION),
                op0=MULT,
                op1=ADD,
            )

        def store(half, bank):
            cols_of = slice(half * HALF, (half + 1) * HALF)
            back_ps = psum.tile([P, HALF_BLOCKS, BLOCK], F32, tag=bank, name="back%d" % half)
            for b, j in enumerate(blocks_of(half)):
                nc.tensor.transpose(back_ps[:, b, :], mixed[:, j, :], ident_f32[:])
            nc.scalar.mul(out=out_sb[:, cols_of], in_=back_ps[:].rearrange("p b m -> p (b m)"), mul=1.0 - SYNC)
            nc.sync.dma_start(out=out[:, cols_of], in_=out_sb[:, cols_of])

        by_vector = nc.vector.tensor_copy
        by_scalar = nc.scalar.copy

        transpose_activations()
        regroup(by_vector, R, 0)
        regroup(by_scalar, R, 1)
        small_vectors()
        quantise_activations()
        transpose_hiddens()
        quantise(R, 0)
        quantise(R, 1)
        regroup(by_vector, Z, 0)
        regroup(by_scalar, Z, 1)
        quantise(Z, 0)
        quantise(Z, 1)
        passes_both(R, 0)
        passes_both(R, 1)
        passes_hn()
        passes_both(Z, 0)
        passes_both(Z, 1)
        for j in range(BLOCKS):
            tension_term_of_n(j)
        for j in range(BLOCKS):
            add_tension(R, j)
            gate_r(j)
        regroup(by_vector, N, 1)
        regroup(by_scalar, N, 0)
        for half in range(HALVES):
            for j in blocks_of(half):
                r_times_hn(j)
            rest_of_n(half)
        for j in range(BLOCKS):
            add_tension(Z, j)
            gate_z(j)
        quantise(N, 1)
        passes_in(1)
        quantise(N, 0)
        passes_in(0)
        order = (1, 0)
        for half in order:
            gate_one_minus_z(half)
        for half in order:
            argument_of_n(half)
            candidate(half)
        for half in order:
            z_times_h(half)
        for half in order:
            keep_fresh(half)
        for half in order:
            new_state(half)
        for half in order:
            faction_sums(half)
        for half, bank in zip(order, ("ra", "rb")):
            pull(half)
            store(half, bank)
